import numpy as np
import ml_dtypes


def mxq(x, axis, fmt="e4m3"):
    dtype, down = {"e4m3": (ml_dtypes.float8_e4m3fn, 7), "e5m2": (ml_dtypes.float8_e5m2, 14)}[fmt]
    v = np.moveaxis(np.asarray(x, np.float32).astype(ml_dtypes.bfloat16).astype(np.float64), axis, -1)
    blocks = v.reshape(v.shape[:-1] + (-1, 32))
    amax = np.abs(blocks).max(-1, keepdims=True)
    byte = np.maximum(np.where(amax > 0, np.frexp(amax)[1] - 1 + 127, 0) - down, 1)
    scale = np.exp2(byte - 127.0)
    codes = (blocks / scale).astype(np.float32).astype(dtype).astype(np.float64)
    return np.moveaxis((codes * scale).reshape(v.shape), -1, axis)


WIDE = False


def mx_kscale(k):
    if not WIDE:
        return np.ones(k)
    levels = np.array([30, -30])
    if k % 512:
        return np.exp2(np.random.permutation(np.resize(levels, k // 32))).repeat(32)
    a = np.empty((k // 512, 16))
    for p in range(k // 512):
        a[p, :8] = np.random.permutation(np.resize(levels, 8))
        for g in range(8):
            far = levels[np.abs(levels - a[p, g]) >= 10]
            a[p, g + 8] = far[np.random.randint(len(far))]
    return np.exp2(a.ravel()).repeat(32)


BF16 = ml_dtypes.bfloat16


def bf(x):
    return np.asarray(x, np.float32).astype(BF16)


def f64(x):
    return np.asarray(x).astype(np.float64)


N, S, D, H, O = 4, 256, 1024, 1024, 1024


def elu(v):
    return np.where(v > 0.0, v, np.exp(np.minimum(v, 0.0)) - 1.0)


def setup_inputs():
    s = mx_kscale(D)
    return {"x": bf(np.random.standard_normal((N, S, D)) * s),
            "Wk": bf(np.random.standard_normal((D, H)) / np.sqrt(D) / s[:, None]),
            "bk": bf(np.random.standard_normal(H) * 0.1),
            "Wv": bf(np.random.standard_normal((D, H)) / np.sqrt(D) / s[:, None]),
            "bv": bf(np.random.standard_normal(H) * 0.1)}


def reference(x, Wk, bk, Wv, bv):
    xq = mxq(f64(x), 2, "e5m2")
    keyp = (xq @ mxq(f64(Wk), 0, "e5m2")) + f64(bk)
    value = (xq @ mxq(f64(Wv), 0, "e5m2")) + f64(bv)
    K = elu(keyp) + 1.0
    KV = np.sum(K * value, axis=1)
    Ksum = np.sum(K, axis=1)
    return KV, Ksum

@@ -1,0 +1,200 @@
+from contextlib import ExitStack
+
+import concourse.mybir as mybir
+from concourse.masks import make_identity
+
+F32 = mybir.dt.float32
+BF16 = mybir.dt.bfloat16
+U32 = mybir.dt.uint32
+U8 = mybir.dt.uint8
+FP8X4 = mybir.dt.float8_e5m2_x4
+ACT = mybir.ActivationFunctionType
+ALU = mybir.AluOpType
+
+NB, S, D, H = 4, 256, 1024, 1024
+P = 128
+TOK = NB * S
+FLOPS = 2 * 2 * TOK * D * H
+
+CG = 512
+CV = (256, 160)
+XV = (3, 7)
+
+
+def tile_linearattention_pa_kernel(tc, x, Wk, bk, Wv, bv, out_0, out_1):
+    nc = tc.nc
+    W = (Wk, Wv)
+    xf = x.flatten_outer_dims()
+
+    with ExitStack() as ctx:
+        keep = ctx.enter_context(tc.tile_pool(name="keep", bufs=1))
+        work = ctx.enter_context(tc.tile_pool(name="work", bufs=3))
+        psum = ctx.enter_context(tc.psum_pool(name="psum", bufs=8))
+
+        warm = keep.tile([P, 1], F32, name="warm")
+        nc.vector.memset(warm[:], 0.0)
+        warm2 = keep.tile([P, 1], F32, name="warm2")
+        nc.scalar.activation(out=warm2[:], in_=warm[:], func=ACT.Exp)
+
+        brow = keep.tile([P, P], BF16, name="brow")
+        nc.gpsimd.memset(brow[:], 0.0)
+        nc.scalar.dma_start(out=brow[0:8, :], in_=bk.rearrange("(t p) -> t p", p=P))
+        nc.scalar.dma_start(out=brow[8:16, :], in_=bv.rearrange("(t p) -> t p", p=P))
+        ident = keep.tile([P, P], F32, name="ident")
+        make_identity(nc, ident[:])
+        res = keep.tile([P, P], F32, name="res")
+        nc.vector.memset(res[:], 0.0)
+
+        raw = {}
+        x_sb = {}
+
+        def load_w(cg):
+            for g in range(2):
+                for m in range(2):
+                    t = keep.tile([P, 4, CG], BF16, name="raw_%d_%d_%d" % (m, g, cg))
+                    nc.sync.dma_start(
+                        out=t[:],
+                        in_=W[m][g * 512 : (g + 1) * 512, cg * CG : (cg + 1) * CG].rearrange("(p j) c -> p j c", j=4),
+                    )
+                    raw[(m, g, cg)] = t
+
+        load_w(0)
+        for r in range(8):
+            t = keep.tile([P, D], BF16, name="x_%d" % r)
+            nc.sync.dma_start(out=t[:], in_=xf[r * P : (r + 1) * P, :])
+            x_sb[r] = t
+        load_w(1)
+
+        wg = {}
+        wc = {}
+        ws = {}
+
+        def interleave_w(m, g, cg):
+            cv = CV[cg]
+            t = keep.tile([P, CG, 4], BF16, name="wg_%d_%d_%d" % (m, g, cg), align_bytes=64)
+            src = raw[(m, g, cg)]
+            nc.vector.tensor_copy(out=t[:, 0:cv, :], in_=src[:, :, 0:cv].rearrange("p j c -> p c j"))
+            nc.scalar.copy(out=t[:, cv:CG, :], in_=src[:, :, cv:CG].rearrange("p j c -> p c j"))
+            wg[(m, g, cg)] = t
+
+        def quantize_w(m, g, cg):
+            codes = keep.tile([P, CG], U32, name="wc_%d_%d_%d" % (m, g, cg), align_bytes=64)
+            scales = keep.tile([P, CG], U8, name="ws_%d_%d_%d" % (m, g, cg), align_bytes=64)
+            nc.vector.quantize_mx(
+                out=codes[:].bitcast(FP8X4),
+                scales=scales[:],
+                in_=wg[(m, g, cg)][:].rearrange("p c j -> p (c j)"),
+            )
+            wc[(m, g, cg)] = codes
+            ws[(m, g, cg)] = scales
+
+        units = [(m, g) for g in range(2) for m in range(2)]
+
+        interleave_w(units[0][0], units[0][1], 0)
+        for i in range(1, 4):
+            interleave_w(units[i][0], units[i][1], 0)
+            quantize_w(units[i - 1][0], units[i - 1][1], 0)
+        quantize_w(units[3][0], units[3][1], 0)
+
+        bf32 = keep.tile([P, P], F32, name="bf32")
+        nc.vector.tensor_copy(out=bf32[:], in_=brow[:])
+        bt = psum.tile([P, 512], F32, tag="bank", name="bt")
+        nc.tensor.transpose(bt[:, 0:P], bf32[:], ident[:])
+        bias = keep.tile([P, 16], F32, name="bias")
+        nc.vector.tensor_copy(out=bias[:], in_=bt[:, 0:16])
+
+        xg = {}
+        xc = {}
+        xs = {}
+        for tg in range(2):
+            for g in range(2):
+                xg[(tg, g)] = keep.tile([P, 2048], BF16, name="xg_%d_%d" % (tg, g), align_bytes=64)
+                xc[(tg, g)] = keep.tile([P, 512], U32, name="xc_%d_%d" % (tg, g), align_bytes=64)
+                xs[(tg, g)] = keep.tile([P, 512], U8, name="xs_%d_%d" % (tg, g), align_bytes=64)
+
+        def x_bank(tg, a, g, idx):
+            xt = psum.tile([P, 512], F32, tag="bank", name="xt")
+            for aa in range(2):
+                words = x_sb[tg * 4 + a * 2 + aa][:].bitcast(F32)
+                for u in range(2):
+                    nc.tensor.transpose(
+                        xt[:, (aa * 2 + u) * P : (aa * 2 + u + 1) * P],
+                        words[:, 256 * g + u : 256 * (g + 1) : 2],
+                        ident[:],
+                    )
+            dst = xg[(tg, g)][:].bitcast(F32)[:, a * 512 : (a + 1) * 512].rearrange("p (a r u) -> p a r u", a=2, u=2)
+            src = xt[:].rearrange("p (a u r) -> p a r u", a=2, u=2)
+            if idx in XV:
+                nc.vector.tensor_copy(out=dst, in_=src)
+            else:
+                nc.scalar.copy(out=dst, in_=src)
+
+        def x_quant(tg, a, g):
+            nc.vector.quantize_mx(
+                out=xc[(tg, g)][:, a * 256 : (a + 1) * 256].bitcast(FP8X4),
+                scales=xs[(tg, g)][:, a * 256 : (a + 1) * 256],
+                in_=xg[(tg, g)][:, a * 1024 : (a + 1) * 1024],
+            )
+
+        idx = 0
+        for tg in range(2):
+            for a in range(2):
+                for g in range(2):
+                    x_bank(tg, a, g, idx)
+                    idx += 1
+                for g in range(2):
+                    x_quant(tg, a, g)
+
+        def pair(ht, tg):
+            cg, c0 = divmod(ht * P, CG)
+            acc = []
+            for m in range(2):
+                t = psum.tile([P, 512], F32, tag="bank", name="acc")
+                for g in range(2):
+                    nc.tensor.matmul_mx(
+                        out=t[:],
+                        lhsT=wc[(m, g, cg)][:, c0 : c0 + P].bitcast(FP8X4),
+                        lhsT_scale=ws[(m, g, cg)][:, c0 : c0 + P],
+                        rhs=xc[(tg, g)][:].bitcast(FP8X4),
+                        rhs_scale=xs[(tg, g)][:],
+                        start=(g == 0),
+                        stop=(g == 1),
+                    )
+                acc.append(t)
+            e = work.tile([P, 512], F32, name="e")
+            nc.scalar.activation(out=e[:], in_=acc[0][:], func=ACT.Exp, bias=bias[:, ht : ht + 1], scale=1.0)
+            r = work.tile([P, 512], F32, name="r")
+            nc.scalar.activation(out=r[:], in_=acc[0][:], func=ACT.Relu, bias=bias[:, ht : ht + 1], scale=1.0)
+            k = work.tile([P, 512], F32, name="k")
+            j = work.tile([P, 512], F32, name="j")
+            for h in range(2):
+                n = tg * 2 + h
+                cols = slice(h * S, (h + 1) * S)
+                nc.vector.scalar_tensor_tensor(
+                    out=k[:, cols], in0=e[:, cols], scalar=1.0, in1=r[:, cols], op0=ALU.min, op1=ALU.add,
+                    accum_out=res[:, 32 + n * 8 + ht : 32 + n * 8 + ht + 1],
+                )
+            for h in range(2):
+                n = tg * 2 + h
+                cols = slice(h * S, (h + 1) * S)
+                nc.vector.scalar_tensor_tensor(
+                    out=j[:, cols], in0=acc[1][:, cols], scalar=bias[:, 8 + ht : 9 + ht], in1=k[:, cols],
+                    op0=ALU.add, op1=ALU.mult,
+                    accum_out=res[:, n * 8 + ht : n * 8 + ht + 1],
+                )
+
+        late = 0
+        for ht in range(8):
+            for tg in range(2):
+                pair(ht, tg)
+            if late < 4:
+                interleave_w(units[late][0], units[late][1], 1)
+                quantize_w(units[late][0], units[late][1], 1)
+                late += 1
+
+        rt = psum.tile([P, 512], F32, tag="bank", name="rt")
+        nc.tensor.transpose(rt[:, 0:P], res[:], ident[:])
+        rs = keep.tile([64, P], F32, name="rs")
+        nc.vector.tensor_copy(out=rs[:], in_=rt[0:64, 0:P])
+        nc.sync.dma_start(out=out_0.rearrange("n (t p) -> (n t) p", p=P), in_=rs[0:32, :])
+        nc.scalar.dma_start(out=out_1.rearrange("n (t p) -> (n t) p", p=P), in_=rs[32:64, :])

@@ -16,9 +16,22 @@ P = 128
 TOK = NB * S
 FLOPS = 2 * 2 * TOK * D * H
 
-CG = 512
-CV = (256, 160)
-XV = (3, 7)
+MANUAL = True
+WARM = 4
+CVD = 160
+ACC_BUFS = 8
+FE_BUFS = 2
+DUM = 2
+PAIRS = [(ht, tg) for tg in range(2) for ht in range(8)]
+ORDER = (
+    ["btr", "xt000", "xt001", "dm0", "xt010", "xt011", "dm1", "mx0_0", "mx1_0", "wm10", "mx0_1", "mx1_1", "wm11", "wm12", "wm13", "wm20", "mx2_0", "mx3_0", "wm21", "mx2_1", "wm22", "mx3_1", "wm30", "wm23", "wm31", "wm32", "wm33", "mx4_0", "mx4_1", "mx5_0", "mx5_1", "xt100", "xt101", "xt110", "xt111", "mx6_0", "mx6_1", "mx7_0", "mx7_1", "mx8_0", "mx8_1", "mx9_0", "mx9_1", "mx10_0", "mx10_1", "mx11_0", "mx11_1", "mx12_0", "mx12_1", "mx13_0", "mx13_1", "mx14_0", "mx14_1", "mx15_0", "mx15_1"],
+    ["xc000", "wdS00", "xc010", "wdS01", "wdS02", "wdS03", "exp0", "relu0", "exp1", "relu1", "w10", "w11", "w12", "w13", "w20", "exp2", "relu2", "w21", "exp3", "w22", "relu3", "w30", "w23", "w31", "w32", "w33", "exp4", "relu4", "exp5", "relu5", "xc100", "xc101", "xc110", "xc111", "exp6", "relu6", "exp7", "relu7", "exp8", "relu8", "exp9", "relu9", "exp10", "relu10", "exp11", "relu11", "exp12", "relu12", "exp13", "relu13", "exp14", "relu14", "exp15", "relu15"],
+    ["identb", "bcast", "bout", "xc001", "xq000", "xq010", "wdV00", "wdV01", "xc011", "xq001", "xq011", "wq00", "wq01", "wdV02", "wdV03", "wq02", "wq03", "vk0", "vp0", "vk1", "wq10", "vp1", "wq11", "vk2", "wq20", "vp2", "vk3", "vp3", "wq21", "wq30", "wq31", "vk4", "vp4", "vk5", "vp5", "xq10", "xq11", "vk6", "vp6", "vk7", "vk8", "vp7", "vp8", "vk9", "vk10", "vp9", "vp10", "vk11", "vk12", "vp11", "vp12", "vk13", "vk14", "vp13", "vp14", "vk15", "vp15"],
+)
+
+
+def mark(key):
+    return None
 
 
 def tile_linearattention_pa_kernel(tc, x, Wk, bk, Wv, bv, out_0, out_1):
@@ -29,79 +42,64 @@ def tile_linearattention_pa_kernel(tc, x, Wk, bk, Wv, bv, out_0, out_1):
     with ExitStack() as ctx:
         keep = ctx.enter_context(tc.tile_pool(name="keep", bufs=1))
         work = ctx.enter_context(tc.tile_pool(name="work", bufs=3))
-        psum = ctx.enter_context(tc.psum_pool(name="psum", bufs=8))
-
-        warm = keep.tile([P, 1], F32, name="warm")
-        nc.vector.memset(warm[:], 0.0)
-        warm2 = keep.tile([P, 1], F32, name="warm2")
-        nc.scalar.activation(out=warm2[:], in_=warm[:], func=ACT.Exp)
+        psum = ctx.enter_context(tc.psum_pool(name="psum", bufs=1))
+        if MANUAL:
+            ctx.enter_context(tc.manual_schedule())
 
         brow = keep.tile([P, P], BF16, name="brow")
         nc.gpsimd.memset(brow[:], 0.0)
         nc.scalar.dma_start(out=brow[0:8, :], in_=bk.rearrange("(t p) -> t p", p=P))
         nc.scalar.dma_start(out=brow[8:16, :], in_=bv.rearrange("(t p) -> t p", p=P))
+
+        x_sb = {}
+        raw = {}
+
+        def load_x(tg):
+            for r in range(tg * 4, tg * 4 + 4):
+                t = keep.tile([P, D], BF16, name="x_%d" % r)
+                nc.sync.dma_start(out=t[:], in_=xf[r * P : (r + 1) * P, :])
+                x_sb[r] = t
+
+        def load_w(c_first, n_c):
+            width = 256 * n_c
+            for q in range(4):
+                m, g = divmod(q, 2)
+                t = keep.tile([P, 4, width], BF16, name="raw_%d_%d" % (c_first, q))
+                nc.sync.dma_start(
+                    out=t[:],
+                    in_=W[m][g * 512 : (g + 1) * 512, c_first * 256 : c_first * 256 + width].rearrange("(p j) c -> p j c", j=4),
+                )
+                for i in range(n_c):
+                    raw[(c_first + i, q)] = t[:, :, i * 256 : (i + 1) * 256]
+
+        load_x(0)
+        load_w(0, 1)
+        load_w(1, 1)
+        load_w(2, 2)
+        load_x(1)
+
+        warm = keep.tile([P, 1], F32, name="warm")
+        nc.vector.memset(warm[:], 0.0)
+        warm2 = keep.tile([P, 1], F32, name="warm2")
+        nc.scalar.activation(out=warm2[:], in_=warm[:], func=ACT.Exp)
         ident = keep.tile([P, P], F32, name="ident")
         make_identity(nc, ident[:])
+        identb = keep.tile([P, P], BF16, name="identb")
         res = keep.tile([P, P], F32, name="res")
         nc.vector.memset(res[:], 0.0)
+        if WARM:
+            dq = keep.tile([P, 2048], BF16, name="dq", align_bytes=64)
+            nc.vector.memset(dq[:], 1.0)
+            dc = keep.tile([P, 512], U32, name="dc", align_bytes=64)
+            ds = keep.tile([P, 512], U8, name="ds", align_bytes=64)
+            nc.vector.quantize_mx(out=dc[:].bitcast(FP8X4), scales=ds[:], in_=dq[:])
+            dps = psum.tile([P, 512], F32, tag="acc", bufs=ACC_BUFS, name="dps")
+            for i in range(WARM):
+                nc.tensor.matmul_mx(out=dps[:], lhsT=dc[:, 0:P].bitcast(FP8X4), lhsT_scale=ds[:, 0:P],
+                                    rhs=dc[:].bitcast(FP8X4), rhs_scale=ds[:], start=True, stop=True)
 
-        raw = {}
-        x_sb = {}
-
-        def load_w(cg):
-            for g in range(2):
-                for m in range(2):
-                    t = keep.tile([P, 4, CG], BF16, name="raw_%d_%d_%d" % (m, g, cg))
-                    nc.sync.dma_start(
-                        out=t[:],
-                        in_=W[m][g * 512 : (g + 1) * 512, cg * CG : (cg + 1) * CG].rearrange("(p j) c -> p j c", j=4),
-                    )
-                    raw[(m, g, cg)] = t
-
-        load_w(0)
-        for r in range(8):
-            t = keep.tile([P, D], BF16, name="x_%d" % r)
-            nc.sync.dma_start(out=t[:], in_=xf[r * P : (r + 1) * P, :])
-            x_sb[r] = t
-        load_w(1)
-
-        wg = {}
-        wc = {}
-        ws = {}
-
-        def interleave_w(m, g, cg):
-            cv = CV[cg]
-            t = keep.tile([P, CG, 4], BF16, name="wg_%d_%d_%d" % (m, g, cg), align_bytes=64)
-            src = raw[(m, g, cg)]
-            nc.vector.tensor_copy(out=t[:, 0:cv, :], in_=src[:, :, 0:cv].rearrange("p j c -> p c j"))
-            nc.scalar.copy(out=t[:, cv:CG, :], in_=src[:, :, cv:CG].rearrange("p j c -> p c j"))
-            wg[(m, g, cg)] = t
-
-        def quantize_w(m, g, cg):
-            codes = keep.tile([P, CG], U32, name="wc_%d_%d_%d" % (m, g, cg), align_bytes=64)
-            scales = keep.tile([P, CG], U8, name="ws_%d_%d_%d" % (m, g, cg), align_bytes=64)
-            nc.vector.quantize_mx(
-                out=codes[:].bitcast(FP8X4),
-                scales=scales[:],
-                in_=wg[(m, g, cg)][:].rearrange("p c j -> p (c j)"),
-            )
-            wc[(m, g, cg)] = codes
-            ws[(m, g, cg)] = scales
-
-        units = [(m, g) for g in range(2) for m in range(2)]
-
-        interleave_w(units[0][0], units[0][1], 0)
-        for i in range(1, 4):
-            interleave_w(units[i][0], units[i][1], 0)
-            quantize_w(units[i - 1][0], units[i - 1][1], 0)
-        quantize_w(units[3][0], units[3][1], 0)
-
-        bf32 = keep.tile([P, P], F32, name="bf32")
-        nc.vector.tensor_copy(out=bf32[:], in_=brow[:])
-        bt = psum.tile([P, 512], F32, tag="bank", name="bt")
-        nc.tensor.transpose(bt[:, 0:P], bf32[:], ident[:])
         bias = keep.tile([P, 16], F32, name="bias")
-        nc.vector.tensor_copy(out=bias[:], in_=bt[:, 0:16])
+        bf32 = keep.tile([P, P], F32, name="bf32")
 
         xg = {}
         xc = {}
@@ -111,90 +109,233 @@ def tile_linearattention_pa_kernel(tc, x, Wk, bk, Wv, bv, out_0, out_1):
                 xg[(tg, g)] = keep.tile([P, 2048], BF16, name="xg_%d_%d" % (tg, g), align_bytes=64)
                 xc[(tg, g)] = keep.tile([P, 512], U32, name="xc_%d_%d" % (tg, g), align_bytes=64)
                 xs[(tg, g)] = keep.tile([P, 512], U8, name="xs_%d_%d" % (tg, g), align_bytes=64)
+        wg = {}
+        wc = {}
+        ws = {}
+        for c in range(4):
+            wg[c] = keep.tile([P, 4, 1024], BF16, name="wg_%d" % c, align_bytes=64)
+            wc[c] = keep.tile([P, 4, 256], U32, name="wc_%d" % c, align_bytes=64)
+            ws[c] = keep.tile([P, 4, 256], U8, name="ws_%d" % c, align_bytes=64)
 
-        def x_bank(tg, a, g, idx):
-            xt = psum.tile([P, 512], F32, tag="bank", name="xt")
+        live = {}
+
+        def t_dummy(k):
+            dps2 = psum.tile([P, 512], F32, tag="acc", bufs=ACC_BUFS, name="dps2")
+            for i in range(k):
+                nc.tensor.matmul_mx(out=dps2[:], lhsT=dc[:, 0:P].bitcast(FP8X4), lhsT_scale=ds[:, 0:P],
+                                    rhs=dc[:].bitcast(FP8X4), rhs_scale=ds[:], start=True, stop=True)
+
+        def t_identb():
+            nc.vector.tensor_copy(out=identb[:], in_=ident[:])
+
+        def t_bias_cast():
+            nc.vector.tensor_copy(out=bf32[:], in_=brow[:])
+
+        def t_bias_tr():
+            bt = psum.tile([P, 512], F32, tag="acc", bufs=ACC_BUFS, name="bt")
+            nc.tensor.transpose(bt[:, 0:P], bf32[:], ident[:])
+            live["bt"] = bt
+
+        def t_bias_out():
+            nc.vector.tensor_copy(out=bias[:], in_=live["bt"][:, 0:16])
+
+        def t_xt(tg, a, g):
+            xt = psum.tile([P, 512], F32, tag="acc", bufs=ACC_BUFS, name="xt")
             for aa in range(2):
                 words = x_sb[tg * 4 + a * 2 + aa][:].bitcast(F32)
                 for u in range(2):
-                    nc.tensor.transpose(
-                        xt[:, (aa * 2 + u) * P : (aa * 2 + u + 1) * P],
-                        words[:, 256 * g + u : 256 * (g + 1) : 2],
-                        ident[:],
-                    )
+                    nc.tensor.transpose(xt[:, (aa * 2 + u) * P : (aa * 2 + u + 1) * P],
+                                        words[:, 256 * g + u : 256 * (g + 1) : 2], ident[:])
+            live[("xt", tg, a, g)] = xt
+
+        def t_xc(eng, tg, a, g):
             dst = xg[(tg, g)][:].bitcast(F32)[:, a * 512 : (a + 1) * 512].rearrange("p (a r u) -> p a r u", a=2, u=2)
-            src = xt[:].rearrange("p (a u r) -> p a r u", a=2, u=2)
-            if idx in XV:
+            src = live[("xt", tg, a, g)][:].rearrange("p (a u r) -> p a r u", a=2, u=2)
+            if eng == "V":
                 nc.vector.tensor_copy(out=dst, in_=src)
             else:
                 nc.scalar.copy(out=dst, in_=src)
 
-        def x_quant(tg, a, g):
+        def t_xq(tg, g, a0, na):
             nc.vector.quantize_mx(
-                out=xc[(tg, g)][:, a * 256 : (a + 1) * 256].bitcast(FP8X4),
-                scales=xs[(tg, g)][:, a * 256 : (a + 1) * 256],
-                in_=xg[(tg, g)][:, a * 1024 : (a + 1) * 1024],
+                out=xc[(tg, g)][:, a0 * 256 : (a0 + na) * 256].bitcast(FP8X4),
+                scales=xs[(tg, g)][:, a0 * 256 : (a0 + na) * 256],
+                in_=xg[(tg, g)][:, a0 * 1024 : (a0 + na) * 1024],
             )
 
-        idx = 0
-        for tg in range(2):
-            for a in range(2):
-                for g in range(2):
-                    x_bank(tg, a, g, idx)
-                    idx += 1
-                for g in range(2):
-                    x_quant(tg, a, g)
+        def t_wd(eng, c, q):
+            src = raw[(c, q)]
+            dst = wg[c][:, q, :].rearrange("p (c j) -> p c j", j=4)
+            if eng == "V":
+                nc.vector.tensor_copy(out=dst[:, 0:CVD, :], in_=src[:, :, 0:CVD].rearrange("p j c -> p c j"))
+            else:
+                nc.scalar.copy(out=dst[:, CVD:256, :], in_=src[:, :, CVD:256].rearrange("p j c -> p c j"))
 
-        def pair(ht, tg):
-            cg, c0 = divmod(ht * P, CG)
-            acc = []
-            for m in range(2):
-                t = psum.tile([P, 512], F32, tag="bank", name="acc")
-                for g in range(2):
-                    nc.tensor.matmul_mx(
-                        out=t[:],
-                        lhsT=wc[(m, g, cg)][:, c0 : c0 + P].bitcast(FP8X4),
-                        lhsT_scale=ws[(m, g, cg)][:, c0 : c0 + P],
-                        rhs=xc[(tg, g)][:].bitcast(FP8X4),
-                        rhs_scale=xs[(tg, g)][:],
-                        start=(g == 0),
-                        stop=(g == 1),
-                    )
-                acc.append(t)
+        def t_wm(c, q):
+            wt = psum.tile([P, 1024], BF16, tag="acc", bufs=ACC_BUFS, name="wt")
+            for i in range(2):
+                nc.tensor.matmul(out=wt[:, i * 512 : (i + 1) * 512], lhsT=identb[:],
+                                 rhs=raw[(c, q)][:, :, i * P : (i + 1) * P].rearrange("p j c -> p c j"),
+                                 start=True, stop=True)
+            live[("wt", c, q)] = wt
+
+        def t_wc(eng, c, q):
+            if eng == "V":
+                nc.vector.tensor_copy(out=wg[c][:, q, :], in_=live[("wt", c, q)][:])
+            else:
+                nc.scalar.copy(out=wg[c][:, q, :], in_=live[("wt", c, q)][:])
+
+        def t_wq(c, q0, nq):
+            nc.vector.quantize_mx(
+                out=wc[c][:, q0 : q0 + nq, :].rearrange("p q c -> p (q c)").bitcast(FP8X4),
+                scales=ws[c][:, q0 : q0 + nq, :].rearrange("p q c -> p (q c)"),
+                in_=wg[c][:, q0 : q0 + nq, :].rearrange("p q c -> p (q c)"),
+            )
+
+        def t_mx(n, m):
+            ht, tg = PAIRS[n]
+            c, hh = divmod(ht, 2)
+            t = psum.tile([P, 512], F32, tag="acc", bufs=ACC_BUFS, name="acc")
+            for g in range(2):
+                nc.tensor.matmul_mx(
+                    out=t[:],
+                    lhsT=wc[c][:, m * 2 + g, hh * P : (hh + 1) * P].bitcast(FP8X4),
+                    lhsT_scale=ws[c][:, m * 2 + g, hh * P : (hh + 1) * P],
+                    rhs=xc[(tg, g)][:].bitcast(FP8X4),
+                    rhs_scale=xs[(tg, g)][:],
+                    start=(g == 0), stop=(g == 1),
+                )
+            live[("acc", n, m)] = t
+
+        def t_exp(n):
+            ht = PAIRS[n][0]
             e = work.tile([P, 512], F32, name="e")
-            nc.scalar.activation(out=e[:], in_=acc[0][:], func=ACT.Exp, bias=bias[:, ht : ht + 1], scale=1.0)
+            nc.scalar.activation(out=e[:], in_=live[("acc", n, 0)][:], func=ACT.Exp, bias=bias[:, ht : ht + 1], scale=1.0)
+            live[("e", n)] = e
+
+        def t_relu(n):
+            ht = PAIRS[n][0]
             r = work.tile([P, 512], F32, name="r")
-            nc.scalar.activation(out=r[:], in_=acc[0][:], func=ACT.Relu, bias=bias[:, ht : ht + 1], scale=1.0)
+            nc.scalar.activation(out=r[:], in_=live[("acc", n, 0)][:], func=ACT.Relu, bias=bias[:, ht : ht + 1], scale=1.0)
+            live[("r", n)] = r
+
+        def t_vk(n):
+            ht, tg = PAIRS[n]
             k = work.tile([P, 512], F32, name="k")
+            for h in range(2):
+                col = 32 + (tg * 2 + h) * 8 + ht
+                cols = slice(h * S, (h + 1) * S)
+                nc.vector.scalar_tensor_tensor(out=k[:, cols], in0=live[("e", n)][:, cols], scalar=1.0, in1=live[("r", n)][:, cols],
+                                               op0=ALU.min, op1=ALU.add, accum_out=res[:, col : col + 1])
+            live[("k", n)] = k
+
+        def t_vp(n):
+            ht, tg = PAIRS[n]
             j = work.tile([P, 512], F32, name="j")
             for h in range(2):
-                n = tg * 2 + h
+                col = (tg * 2 + h) * 8 + ht
                 cols = slice(h * S, (h + 1) * S)
-                nc.vector.scalar_tensor_tensor(
-                    out=k[:, cols], in0=e[:, cols], scalar=1.0, in1=r[:, cols], op0=ALU.min, op1=ALU.add,
-                    accum_out=res[:, 32 + n * 8 + ht : 32 + n * 8 + ht + 1],
-                )
-            for h in range(2):
-                n = tg * 2 + h
-                cols = slice(h * S, (h + 1) * S)
-                nc.vector.scalar_tensor_tensor(
-                    out=j[:, cols], in0=acc[1][:, cols], scalar=bias[:, 8 + ht : 9 + ht], in1=k[:, cols],
-                    op0=ALU.add, op1=ALU.mult,
-                    accum_out=res[:, n * 8 + ht : n * 8 + ht + 1],
-                )
+                nc.vector.scalar_tensor_tensor(out=j[:, cols], in0=live[("acc", n, 1)][:, cols], scalar=bias[:, 8 + ht : 9 + ht],
+                                               in1=live[("k", n)][:, cols], op0=ALU.add, op1=ALU.mult,
+                                               accum_out=res[:, col : col + 1])
 
-        late = 0
-        for ht in range(8):
-            for tg in range(2):
-                pair(ht, tg)
-            if late < 4:
-                interleave_w(units[late][0], units[late][1], 1)
-                quantize_w(units[late][0], units[late][1], 1)
-                late += 1
+        tasks = {}
+        text = []
 
-        rt = psum.tile([P, 512], F32, tag="bank", name="rt")
+        def add(key, eng, fn, args, deps):
+            tasks[key] = (eng, fn, args, deps)
+            text.append(key)
+
+        def fe_x(tg, engs, fine):
+            for a in range(2):
+                for g in range(2):
+                    add("xt%d%d%d" % (tg, a, g), "T", t_xt, (tg, a, g), [])
+                    add("xc%d%d%d" % (tg, a, g), engs[a * 2 + g], t_xc, (engs[a * 2 + g], tg, a, g), ["xt%d%d%d" % (tg, a, g)])
+                if fine:
+                    if DUM:
+                        add("dm%d" % a, "T", t_dummy, (DUM,), [])
+                    for g in range(2):
+                        add("xq%d%d%d" % (tg, g, a), "V", t_xq, (tg, g, a, 1), ["xc%d%d%d" % (tg, a, g)])
+            if not fine:
+                for g in range(2):
+                    add("xq%d%d" % (tg, g), "V", t_xq, (tg, g, 0, 2), ["xc%d%d%d" % (tg, a, g) for a in range(2)])
+
+        def fe_w(c, engs, fine):
+            for q in range(4):
+                if c > 0:
+                    add("wm%d%d" % (c, q), "T", t_wm, (c, q), ["identb"])
+                    add("w%d%d" % (c, q), engs[q], t_wc, (engs[q], c, q), ["wm%d%d" % (c, q)])
+                    got = ["w%d%d" % (c, q)]
+                else:
+                    add("wdS%d%d" % (c, q), "S", t_wd, ("S", c, q), [])
+                    add("wdV%d%d" % (c, q), "V", t_wd, ("V", c, q), [])
+                    got = ["wdS%d%d" % (c, q), "wdV%d%d" % (c, q)]
+                if fine:
+                    add("wq%d%d" % (c, q), "V", t_wq, (c, q, 1), got)
+                elif q % 2 == 1:
+                    add("wq%d%d" % (c, q // 2), "V", t_wq, (c, q - 1, 2), got + ["w%d%d" % (c, q - 1)])
+
+        FINE_X = (True, False)
+        FINE_W = (True, False, False, False)
+
+        def need(n, m):
+            ht, tg = PAIRS[n]
+            c = ht // 2
+            d = ["xq%d%d%d" % (tg, g, a) for g in range(2) for a in range(2)] if FINE_X[tg] else ["xq%d%d" % (tg, g) for g in range(2)]
+            return d + (["wq%d%d" % (c, m * 2 + g) for g in range(2)] if FINE_W[c] else ["wq%d%d" % (c, m)])
+
+        def pair(n):
+            for m in range(2):
+                add("mx%d_%d" % (n, m), "T", t_mx, (n, m), need(n, m))
+            add("exp%d" % n, "S", t_exp, (n,), ["mx%d_0" % n, "bout"])
+            add("relu%d" % n, "S", t_relu, (n,), ["mx%d_0" % n, "bout"])
+            add("vk%d" % n, "V", t_vk, (n,), ["exp%d" % n, "relu%d" % n])
+            add("vp%d" % n, "V", t_vp, (n,), ["vk%d" % n, "mx%d_1" % n])
+
+        add("identb", "V", t_identb, (), [])
+        add("bcast", "V", t_bias_cast, (), [])
+        add("btr", "T", t_bias_tr, (), ["bcast"])
+        add("bout", "V", t_bias_out, (), ["btr"])
+        fe_x(0, ("S", "V", "S", "V"), FINE_X[0])
+        fe_w(0, ("S", "V", "S", "S"), FINE_W[0])
+        pair(0)
+        pair(1)
+        fe_w(1, ("S", "S", "S", "S"), FINE_W[1])
+        fe_w(2, ("S", "S", "S", "S"), FINE_W[2])
+        pair(2)
+        pair(3)
+        fe_w(3, ("S", "S", "S", "S"), FINE_W[3])
+        pair(4)
+        pair(5)
+        fe_x(1, ("S", "S", "S", "S"), FINE_X[1])
+        for n in range(6, 16):
+            pair(n)
+
+        if ORDER is None:
+            for key in text:
+                mark(key)
+                tasks[key][1](*tasks[key][2])
+        else:
+            done = set()
+            pos = [0, 0, 0]
+            while len(done) < len(text):
+                moved = False
+                for i in range(3):
+                    while pos[i] < len(ORDER[i]):
+                        key = ORDER[i][pos[i]]
+                        if not all(d in done for d in tasks[key][3]):
+                            break
+                        mark(key)
+                        tasks[key][1](*tasks[key][2])
+                        done.add(key)
+                        pos[i] += 1
+                        moved = True
+                assert moved, "the three orders contradict each other"
+        mark(None)
+
+        rt = psum.tile([P, 512], F32, tag="acc", bufs=ACC_BUFS, name="rt")
         nc.tensor.transpose(rt[:, 0:P], res[:], ident[:])
         rs = keep.tile([64, P], F32, name="rs")
-        nc.vector.tensor_copy(out=rs[:], in_=rt[0:64, 0:P])
+        nc.scalar.copy(out=rs[:], in_=rt[0:64, 0:P])
         nc.sync.dma_start(out=out_0.rearrange("n (t p) -> (n t) p", p=P), in_=rs[0:32, :])
         nc.scalar.dma_start(out=out_1.rearrange("n (t p) -> (n t) p", p=P), in_=rs[32:64, :])

@@ -16,18 +16,12 @@ P = 128
 TOK = NB * S
 FLOPS = 2 * 2 * TOK * D * H
 
-MANUAL = True
-WARM = 4
-CVD = 160
-ACC_BUFS = 8
-FE_BUFS = 2
-DUM = 2
-PAIRS = [(ht, tg) for tg in range(2) for ht in range(8)]
-ORDER = (
-    ["btr", "xt000", "xt001", "dm0", "xt010", "xt011", "dm1", "mx0_0", "mx1_0", "wm10", "mx0_1", "mx1_1", "wm11", "wm12", "wm13", "wm20", "mx2_0", "mx3_0", "wm21", "mx2_1", "wm22", "mx3_1", "wm30", "wm23", "wm31", "wm32", "wm33", "mx4_0", "mx4_1", "mx5_0", "mx5_1", "xt100", "xt101", "xt110", "xt111", "mx6_0", "mx6_1", "mx7_0", "mx7_1", "mx8_0", "mx8_1", "mx9_0", "mx9_1", "mx10_0", "mx10_1", "mx11_0", "mx11_1", "mx12_0", "mx12_1", "mx13_0", "mx13_1", "mx14_0", "mx14_1", "mx15_0", "mx15_1"],
-    ["xc000", "wdS00", "xc010", "wdS01", "wdS02", "wdS03", "exp0", "relu0", "exp1", "relu1", "w10", "w11", "w12", "w13", "w20", "exp2", "relu2", "w21", "exp3", "w22", "relu3", "w30", "w23", "w31", "w32", "w33", "exp4", "relu4", "exp5", "relu5", "xc100", "xc101", "xc110", "xc111", "exp6", "relu6", "exp7", "relu7", "exp8", "relu8", "exp9", "relu9", "exp10", "relu10", "exp11", "relu11", "exp12", "relu12", "exp13", "relu13", "exp14", "relu14", "exp15", "relu15"],
-    ["identb", "bcast", "bout", "xc001", "xq000", "xq010", "wdV00", "wdV01", "xc011", "xq001", "xq011", "wq00", "wq01", "wdV02", "wdV03", "wq02", "wq03", "vk0", "vp0", "vk1", "wq10", "vp1", "wq11", "vk2", "wq20", "vp2", "vk3", "vp3", "wq21", "wq30", "wq31", "vk4", "vp4", "vk5", "vp5", "xq10", "xq11", "vk6", "vp6", "vk7", "vk8", "vp7", "vp8", "vk9", "vk10", "vp9", "vp10", "vk11", "vk12", "vp11", "vp12", "vk13", "vk14", "vp13", "vp14", "vk15", "vp15"],
-)
+MANUAL = False
+CS = 168
+BANKS = 8
+VUNITS = ((0, 0), (0, 1))
+PAIRS = [(2 * c + hh, tg) for c in range(4) for tg in range(2) for hh in range(2)]
+DTYPE = ()
 
 
 def mark(key):
@@ -74,9 +68,9 @@ def tile_linearattention_pa_kernel(tc, x, Wk, bk, Wv, bv, out_0, out_1):
 
         load_x(0)
         load_w(0, 1)
+        load_x(1)
         load_w(1, 1)
         load_w(2, 2)
-        load_x(1)
 
         warm = keep.tile([P, 1], F32, name="warm")
         nc.vector.memset(warm[:], 0.0)
@@ -84,22 +78,17 @@ def tile_linearattention_pa_kernel(tc, x, Wk, bk, Wv, bv, out_0, out_1):
         nc.scalar.activation(out=warm2[:], in_=warm[:], func=ACT.Exp)
         ident = keep.tile([P, P], F32, name="ident")
         make_identity(nc, ident[:])
-        identb = keep.tile([P, P], BF16, name="identb")
         res = keep.tile([P, P], F32, name="res")
         nc.vector.memset(res[:], 0.0)
-        if WARM:
-            dq = keep.tile([P, 2048], BF16, name="dq", align_bytes=64)
-            nc.vector.memset(dq[:], 1.0)
-            dc = keep.tile([P, 512], U32, name="dc", align_bytes=64)
-            ds = keep.tile([P, 512], U8, name="ds", align_bytes=64)
-            nc.vector.quantize_mx(out=dc[:].bitcast(FP8X4), scales=ds[:], in_=dq[:])
-            dps = psum.tile([P, 512], F32, tag="acc", bufs=ACC_BUFS, name="dps")
-            for i in range(WARM):
-                nc.tensor.matmul_mx(out=dps[:], lhsT=dc[:, 0:P].bitcast(FP8X4), lhsT_scale=ds[:, 0:P],
-                                    rhs=dc[:].bitcast(FP8X4), rhs_scale=ds[:], start=True, stop=True)
 
         bias = keep.tile([P, 16], F32, name="bias")
         bf32 = keep.tile([P, P], F32, name="bf32")
+        bk1 = keep.tile([P, 8], F32, name="bk1")
+        nbk = keep.tile([P, 8], F32, name="nbk")
+        s_e = keep.tile([P, 32], F32, name="s_e")
+        s_r = keep.tile([P, 32], F32, name="s_r")
+        nc.gpsimd.memset(s_e[:], 0.0)
+        nc.gpsimd.memset(s_r[:], 0.0)
 
         xg = {}
         xc = {}
@@ -119,28 +108,21 @@ def tile_linearattention_pa_kernel(tc, x, Wk, bk, Wv, bv, out_0, out_1):
 
         live = {}
 
-        def t_dummy(k):
-            dps2 = psum.tile([P, 512], F32, tag="acc", bufs=ACC_BUFS, name="dps2")
-            for i in range(k):
-                nc.tensor.matmul_mx(out=dps2[:], lhsT=dc[:, 0:P].bitcast(FP8X4), lhsT_scale=ds[:, 0:P],
-                                    rhs=dc[:].bitcast(FP8X4), rhs_scale=ds[:], start=True, stop=True)
-
-        def t_identb():
-            nc.vector.tensor_copy(out=identb[:], in_=ident[:])
-
         def t_bias_cast():
             nc.vector.tensor_copy(out=bf32[:], in_=brow[:])
 
         def t_bias_tr():
-            bt = psum.tile([P, 512], F32, tag="acc", bufs=ACC_BUFS, name="bt")
+            bt = psum.tile([P, 512], F32, tag="bank", bufs=BANKS, name="bt")
             nc.tensor.transpose(bt[:, 0:P], bf32[:], ident[:])
             live["bt"] = bt
 
         def t_bias_out():
             nc.vector.tensor_copy(out=bias[:], in_=live["bt"][:, 0:16])
+            nc.vector.tensor_scalar(out=bk1[:], in0=bias[:, 0:8], scalar1=1.0, scalar2=None, op0=ALU.add)
+            nc.vector.tensor_scalar(out=nbk[:], in0=bias[:, 0:8], scalar1=-1.0, scalar2=None, op0=ALU.mult)
 
         def t_xt(tg, a, g):
-            xt = psum.tile([P, 512], F32, tag="acc", bufs=ACC_BUFS, name="xt")
+            xt = psum.tile([P, 512], F32, tag="bank", bufs=BANKS, name="xt")
             for aa in range(2):
                 words = x_sb[tg * 4 + a * 2 + aa][:].bitcast(F32)
                 for u in range(2):
@@ -167,23 +149,12 @@ def tile_linearattention_pa_kernel(tc, x, Wk, bk, Wv, bv, out_0, out_1):
             src = raw[(c, q)]
             dst = wg[c][:, q, :].rearrange("p (c j) -> p c j", j=4)
             if eng == "V":
-                nc.vector.tensor_copy(out=dst[:, 0:CVD, :], in_=src[:, :, 0:CVD].rearrange("p j c -> p c j"))
+                nc.vector.tensor_copy(out=dst, in_=src.rearrange("p j c -> p c j"))
+            elif eng == "S":
+                nc.scalar.copy(out=dst[:, 0:CS, :], in_=src[:, :, 0:CS].rearrange("p j c -> p c j"))
             else:
-                nc.scalar.copy(out=dst[:, CVD:256, :], in_=src[:, :, CVD:256].rearrange("p j c -> p c j"))
-
-        def t_wm(c, q):
-            wt = psum.tile([P, 1024], BF16, tag="acc", bufs=ACC_BUFS, name="wt")
-            for i in range(2):
-                nc.tensor.matmul(out=wt[:, i * 512 : (i + 1) * 512], lhsT=identb[:],
-                                 rhs=raw[(c, q)][:, :, i * P : (i + 1) * P].rearrange("p j c -> p c j"),
-                                 start=True, stop=True)
-            live[("wt", c, q)] = wt
-
-        def t_wc(eng, c, q):
-            if eng == "V":
-                nc.vector.tensor_copy(out=wg[c][:, q, :], in_=live[("wt", c, q)][:])
-            else:
-                nc.scalar.copy(out=wg[c][:, q, :], in_=live[("wt", c, q)][:])
+                nc.gpsimd.tensor_scalar(out=dst[:, CS:256, :], in0=src[:, :, CS:256].rearrange("p j c -> p c j"),
+                                        scalar1=1.0, scalar2=0.0, op0=ALU.mult, op1=ALU.add)
 
         def t_wq(c, q0, nq):
             nc.vector.quantize_mx(
@@ -195,7 +166,7 @@ def tile_linearattention_pa_kernel(tc, x, Wk, bk, Wv, bv, out_0, out_1):
         def t_mx(n, m):
             ht, tg = PAIRS[n]
             c, hh = divmod(ht, 2)
-            t = psum.tile([P, 512], F32, tag="acc", bufs=ACC_BUFS, name="acc")
+            t = psum.tile([P, 512], F32, tag="bank", bufs=BANKS, name="acc")
             for g in range(2):
                 nc.tensor.matmul_mx(
                     out=t[:],
@@ -213,11 +184,39 @@ def tile_linearattention_pa_kernel(tc, x, Wk, bk, Wv, bv, out_0, out_1):
             nc.scalar.activation(out=e[:], in_=live[("acc", n, 0)][:], func=ACT.Exp, bias=bias[:, ht : ht + 1], scale=1.0)
             live[("e", n)] = e
 
-        def t_relu(n):
-            ht = PAIRS[n][0]
+        def t_d_scalar(n):
+            ht, tg = PAIRS[n]
+            rn = work.tile([P, 512], F32, name="rn")
+            nc.scalar.activation(out=rn[:], in_=live[("acc", n, 0)][:], func=ACT.Relu, bias=nbk[:, ht : ht + 1], scale=-1.0)
+            ec = work.tile([P, 512], F32, name="ec")
             r = work.tile([P, 512], F32, name="r")
-            nc.scalar.activation(out=r[:], in_=live[("acc", n, 0)][:], func=ACT.Relu, bias=bias[:, ht : ht + 1], scale=1.0)
+            for h in range(2):
+                col = (tg * 2 + h) * 8 + ht
+                cols = slice(h * S, (h + 1) * S)
+                nc.scalar.activation(out=r[:, cols], in_=live[("acc", n, 0)][:, cols], func=ACT.Relu, bias=bias[:, ht : ht + 1],
+                                     scale=1.0, accum_out=s_r[:, col : col + 1])
+            for h in range(2):
+                col = (tg * 2 + h) * 8 + ht
+                cols = slice(h * S, (h + 1) * S)
+                nc.scalar.activation(out=ec[:, cols], in_=rn[:, cols], func=ACT.Exp, scale=-1.0, accum_out=s_e[:, col : col + 1])
+            live[("ec", n)] = ec
             live[("r", n)] = r
+
+        def t_d_add(n):
+            k = work.tile([P, 512], F32, name="k")
+            nc.gpsimd.tensor_tensor(out=k[:], in0=live[("ec", n)][:], in1=live[("r", n)][:], op=ALU.add)
+            live[("k", n)] = k
+
+        def t_dsum():
+            nc.vector.tensor_tensor(out=s_e[:], in0=s_e[:], in1=s_r[:], op=ALU.add)
+
+        def t_dres():
+            nc.vector.tensor_tensor(out=res[:, 32:64], in0=res[:, 32:64], in1=s_e[:], op=ALU.add)
+
+        def t_clamp(n):
+            ec = work.tile([P, 512], F32, name="ec")
+            nc.gpsimd.tensor_scalar(out=ec[:], in0=live[("e", n)][:], scalar1=1.0, scalar2=0.0, op0=ALU.min, op1=ALU.max)
+            live[("ec", n)] = ec
 
         def t_vk(n):
             ht, tg = PAIRS[n]
@@ -225,8 +224,9 @@ def tile_linearattention_pa_kernel(tc, x, Wk, bk, Wv, bv, out_0, out_1):
             for h in range(2):
                 col = 32 + (tg * 2 + h) * 8 + ht
                 cols = slice(h * S, (h + 1) * S)
-                nc.vector.scalar_tensor_tensor(out=k[:, cols], in0=live[("e", n)][:, cols], scalar=1.0, in1=live[("r", n)][:, cols],
-                                               op0=ALU.min, op1=ALU.add, accum_out=res[:, col : col + 1])
+                nc.vector.scalar_tensor_tensor(out=k[:, cols], in0=live[("acc", n, 0)][:, cols], scalar=bk1[:, ht : ht + 1],
+                                               in1=live[("ec", n)][:, cols], op0=ALU.add, op1=ALU.max,
+                                               accum_out=res[:, col : col + 1])
             live[("k", n)] = k
 
         def t_vp(n):
@@ -252,28 +252,25 @@ def tile_linearattention_pa_kernel(tc, x, Wk, bk, Wv, bv, out_0, out_1):
                     add("xt%d%d%d" % (tg, a, g), "T", t_xt, (tg, a, g), [])
                     add("xc%d%d%d" % (tg, a, g), engs[a * 2 + g], t_xc, (engs[a * 2 + g], tg, a, g), ["xt%d%d%d" % (tg, a, g)])
                 if fine:
-                    if DUM:
-                        add("dm%d" % a, "T", t_dummy, (DUM,), [])
                     for g in range(2):
                         add("xq%d%d%d" % (tg, g, a), "V", t_xq, (tg, g, a, 1), ["xc%d%d%d" % (tg, a, g)])
             if not fine:
                 for g in range(2):
                     add("xq%d%d" % (tg, g), "V", t_xq, (tg, g, 0, 2), ["xc%d%d%d" % (tg, a, g) for a in range(2)])
 
-        def fe_w(c, engs, fine):
+        def fe_w(c, fine):
             for q in range(4):
-                if c > 0:
-                    add("wm%d%d" % (c, q), "T", t_wm, (c, q), ["identb"])
-                    add("w%d%d" % (c, q), engs[q], t_wc, (engs[q], c, q), ["wm%d%d" % (c, q)])
-                    got = ["w%d%d" % (c, q)]
+                if (c, q) in VUNITS:
+                    add("wdS%d%d" % (c, q), "V", t_wd, ("V", c, q), [])
+                    add("wdG%d%d" % (c, q), "V", mark, (None,), [])
                 else:
                     add("wdS%d%d" % (c, q), "S", t_wd, ("S", c, q), [])
-                    add("wdV%d%d" % (c, q), "V", t_wd, ("V", c, q), [])
-                    got = ["wdS%d%d" % (c, q), "wdV%d%d" % (c, q)]
+                    add("wdG%d%d" % (c, q), "G", t_wd, ("G", c, q), [])
+                got = ["wdS%d%d" % (c, q), "wdG%d%d" % (c, q)]
                 if fine:
                     add("wq%d%d" % (c, q), "V", t_wq, (c, q, 1), got)
                 elif q % 2 == 1:
-                    add("wq%d%d" % (c, q // 2), "V", t_wq, (c, q - 1, 2), got + ["w%d%d" % (c, q - 1)])
+                    add("wq%d%d" % (c, q // 2), "V", t_wq, (c, q - 1, 2), got + ["wdS%d%d" % (c, q - 1), "wdG%d%d" % (c, q - 1)])
 
         FINE_X = (True, False)
         FINE_W = (True, False, False, False)
@@ -287,53 +284,35 @@ def tile_linearattention_pa_kernel(tc, x, Wk, bk, Wv, bv, out_0, out_1):
         def pair(n):
             for m in range(2):
                 add("mx%d_%d" % (n, m), "T", t_mx, (n, m), need(n, m))
-            add("exp%d" % n, "S", t_exp, (n,), ["mx%d_0" % n, "bout"])
-            add("relu%d" % n, "S", t_relu, (n,), ["mx%d_0" % n, "bout"])
-            add("vk%d" % n, "V", t_vk, (n,), ["exp%d" % n, "relu%d" % n])
+            if n in DTYPE:
+                add("ds%d" % n, "S", t_d_scalar, (n,), ["mx%d_0" % n, "bout"])
+                add("vk%d" % n, "G", t_d_add, (n,), ["ds%d" % n])
+            else:
+                add("exp%d" % n, "S", t_exp, (n,), ["mx%d_0" % n, "bout"])
+                add("cl%d" % n, "G", t_clamp, (n,), ["exp%d" % n])
+                add("vk%d" % n, "V", t_vk, (n,), ["cl%d" % n])
+            if n == 15 and len(DTYPE) > 0:
+                add("dsum", "V", t_dsum, (), ["ds%d" % i for i in DTYPE])
+                add("dres", "V", t_dres, (), ["dsum"] + ["vk%d" % i for i in range(16)])
             add("vp%d" % n, "V", t_vp, (n,), ["vk%d" % n, "mx%d_1" % n])
 
-        add("identb", "V", t_identb, (), [])
         add("bcast", "V", t_bias_cast, (), [])
         add("btr", "T", t_bias_tr, (), ["bcast"])
         add("bout", "V", t_bias_out, (), ["btr"])
-        fe_x(0, ("S", "V", "S", "V"), FINE_X[0])
-        fe_w(0, ("S", "V", "S", "S"), FINE_W[0])
-        pair(0)
-        pair(1)
-        fe_w(1, ("S", "S", "S", "S"), FINE_W[1])
-        fe_w(2, ("S", "S", "S", "S"), FINE_W[2])
-        pair(2)
-        pair(3)
-        fe_w(3, ("S", "S", "S", "S"), FINE_W[3])
-        pair(4)
-        pair(5)
+        fe_x(0, ("S", "S", "S", "S"), FINE_X[0])
+        fe_w(0, FINE_W[0])
         fe_x(1, ("S", "S", "S", "S"), FINE_X[1])
-        for n in range(6, 16):
+        for n in range(16):
+            if n % 4 == 2 and n < 12:
+                fe_w(n // 4 + 1, FINE_W[n // 4 + 1])
             pair(n)
 
-        if ORDER is None:
-            for key in text:
-                mark(key)
-                tasks[key][1](*tasks[key][2])
-        else:
-            done = set()
-            pos = [0, 0, 0]
-            while len(done) < len(text):
-                moved = False
-                for i in range(3):
-                    while pos[i] < len(ORDER[i]):
-                        key = ORDER[i][pos[i]]
-                        if not all(d in done for d in tasks[key][3]):
-                            break
-                        mark(key)
-                        tasks[key][1](*tasks[key][2])
-                        done.add(key)
-                        pos[i] += 1
-                        moved = True
-                assert moved, "the three orders contradict each other"
+        for key in text:
+            mark(key)
+            tasks[key][1](*tasks[key][2])
         mark(None)
 
-        rt = psum.tile([P, 512], F32, tag="acc", bufs=ACC_BUFS, name="rt")
+        rt = psum.tile([P, 512], F32, tag="bank", bufs=BANKS, name="rt")
         nc.tensor.transpose(rt[:, 0:P], res[:], ident[:])
         rs = keep.tile([64, P], F32, name="rs")
         nc.scalar.copy(out=rs[:], in_=rt[0:64, 0:P])

@@ -16,16 +16,9 @@ P = 128
 TOK = NB * S
 FLOPS = 2 * 2 * TOK * D * H
 
-MANUAL = False
-CS = 168
-BANKS = 8
-VUNITS = ((0, 0), (0, 1))
-PAIRS = [(2 * c + hh, tg) for c in range(4) for tg in range(2) for hh in range(2)]
-DTYPE = ()
-
-
-def mark(key):
-    return None
+CG = 512
+CV = (256, 160)
+XV = (3, 7)
 
 
 def tile_linearattention_pa_kernel(tc, x, Wk, bk, Wv, bv, out_0, out_1):
@@ -36,59 +29,81 @@ def tile_linearattention_pa_kernel(tc, x, Wk, bk, Wv, bv, out_0, out_1):
     with ExitStack() as ctx:
         keep = ctx.enter_context(tc.tile_pool(name="keep", bufs=1))
         work = ctx.enter_context(tc.tile_pool(name="work", bufs=3))
-        psum = ctx.enter_context(tc.psum_pool(name="psum", bufs=1))
-        if MANUAL:
-            ctx.enter_context(tc.manual_schedule())
-
-        brow = keep.tile([P, P], BF16, name="brow")
-        nc.gpsimd.memset(brow[:], 0.0)
-        nc.scalar.dma_start(out=brow[0:8, :], in_=bk.rearrange("(t p) -> t p", p=P))
-        nc.scalar.dma_start(out=brow[8:16, :], in_=bv.rearrange("(t p) -> t p", p=P))
-
-        x_sb = {}
-        raw = {}
-
-        def load_x(tg):
-            for r in range(tg * 4, tg * 4 + 4):
-                t = keep.tile([P, D], BF16, name="x_%d" % r)
-                nc.sync.dma_start(out=t[:], in_=xf[r * P : (r + 1) * P, :])
-                x_sb[r] = t
-
-        def load_w(c_first, n_c):
-            width = 256 * n_c
-            for q in range(4):
-                m, g = divmod(q, 2)
-                t = keep.tile([P, 4, width], BF16, name="raw_%d_%d" % (c_first, q))
-                nc.sync.dma_start(
-                    out=t[:],
-                    in_=W[m][g * 512 : (g + 1) * 512, c_first * 256 : c_first * 256 + width].rearrange("(p j) c -> p j c", j=4),
-                )
-                for i in range(n_c):
-                    raw[(c_first + i, q)] = t[:, :, i * 256 : (i + 1) * 256]
-
-        load_x(0)
-        load_w(0, 1)
-        load_x(1)
-        load_w(1, 1)
-        load_w(2, 2)
+        psum = ctx.enter_context(tc.psum_pool(name="psum", bufs=8))
 
         warm = keep.tile([P, 1], F32, name="warm")
         nc.vector.memset(warm[:], 0.0)
         warm2 = keep.tile([P, 1], F32, name="warm2")
         nc.scalar.activation(out=warm2[:], in_=warm[:], func=ACT.Exp)
+
+        brow = keep.tile([P, P], BF16, name="brow")
+        nc.gpsimd.memset(brow[:], 0.0)
+        nc.scalar.dma_start(out=brow[0:8, :], in_=bk.rearrange("(t p) -> t p", p=P))
+        nc.scalar.dma_start(out=brow[8:16, :], in_=bv.rearrange("(t p) -> t p", p=P))
         ident = keep.tile([P, P], F32, name="ident")
         make_identity(nc, ident[:])
         res = keep.tile([P, P], F32, name="res")
         nc.vector.memset(res[:], 0.0)
 
-        bias = keep.tile([P, 16], F32, name="bias")
+        raw = {}
+        x_sb = {}
+
+        def load_w(cg):
+            for g in range(2):
+                for m in range(2):
+                    t = keep.tile([P, 4, CG], BF16, name="raw_%d_%d_%d" % (m, g, cg))
+                    nc.sync.dma_start(
+                        out=t[:],
+                        in_=W[m][g * 512 : (g + 1) * 512, cg * CG : (cg + 1) * CG].rearrange("(p j) c -> p j c", j=4),
+                    )
+                    raw[(m, g, cg)] = t
+
+        load_w(0)
+        for r in range(8):
+            t = keep.tile([P, D], BF16, name="x_%d" % r)
+            nc.sync.dma_start(out=t[:], in_=xf[r * P : (r + 1) * P, :])
+            x_sb[r] = t
+        load_w(1)
+
+        wg = {}
+        wc = {}
+        ws = {}
+
+        def interleave_w(m, g, cg):
+            cv = CV[cg]
+            t = keep.tile([P, CG, 4], BF16, name="wg_%d_%d_%d" % (m, g, cg), align_bytes=64)
+            src = raw[(m, g, cg)]
+            nc.vector.tensor_copy(out=t[:, 0:cv, :].rearrange("p (c i) j -> p c j i", i=4),
+                                  in_=src[:, :, 0:cv].rearrange("p j (c i) -> p c j i", i=4))
+            nc.scalar.copy(out=t[:, cv:CG, :].rearrange("p (c i) j -> p c j i", i=4),
+                           in_=src[:, :, cv:CG].rearrange("p j (c i) -> p c j i", i=4))
+            wg[(m, g, cg)] = t
+
+        def quantize_w(m, g, cg):
+            codes = keep.tile([P, CG], U32, name="wc_%d_%d_%d" % (m, g, cg), align_bytes=64)
+            scales = keep.tile([P, CG], U8, name="ws_%d_%d_%d" % (m, g, cg), align_bytes=64)
+            nc.vector.quantize_mx(
+                out=codes[:].bitcast(FP8X4),
+                scales=scales[:],
+                in_=wg[(m, g, cg)][:].rearrange("p c j -> p (c j)"),
+            )
+            wc[(m, g, cg)] = codes
+            ws[(m, g, cg)] = scales
+
+        units = [(m, g) for g in range(2) for m in range(2)]
+
+        interleave_w(units[0][0], units[0][1], 0)
+        for i in range(1, 4):
+            interleave_w(units[i][0], units[i][1], 0)
+            quantize_w(units[i - 1][0], units[i - 1][1], 0)
+        quantize_w(units[3][0], units[3][1], 0)
+
         bf32 = keep.tile([P, P], F32, name="bf32")
-        bk1 = keep.tile([P, 8], F32, name="bk1")
-        nbk = keep.tile([P, 8], F32, name="nbk")
-        s_e = keep.tile([P, 32], F32, name="s_e")
-        s_r = keep.tile([P, 32], F32, name="s_r")
-        nc.gpsimd.memset(s_e[:], 0.0)
-        nc.gpsimd.memset(s_r[:], 0.0)
+        nc.vector.tensor_copy(out=bf32[:], in_=brow[:])
+        bt = psum.tile([P, 512], F32, tag="bank", name="bt")
+        nc.tensor.transpose(bt[:, 0:P], bf32[:], ident[:])
+        bias = keep.tile([P, 16], F32, name="bias")
+        nc.vector.tensor_copy(out=bias[:], in_=bt[:, 0:16])
 
         xg = {}
         xc = {}
@@ -98,223 +113,90 @@ def tile_linearattention_pa_kernel(tc, x, Wk, bk, Wv, bv, out_0, out_1):
                 xg[(tg, g)] = keep.tile([P, 2048], BF16, name="xg_%d_%d" % (tg, g), align_bytes=64)
                 xc[(tg, g)] = keep.tile([P, 512], U32, name="xc_%d_%d" % (tg, g), align_bytes=64)
                 xs[(tg, g)] = keep.tile([P, 512], U8, name="xs_%d_%d" % (tg, g), align_bytes=64)
-        wg = {}
-        wc = {}
-        ws = {}
-        for c in range(4):
-            wg[c] = keep.tile([P, 4, 1024], BF16, name="wg_%d" % c, align_bytes=64)
-            wc[c] = keep.tile([P, 4, 256], U32, name="wc_%d" % c, align_bytes=64)
-            ws[c] = keep.tile([P, 4, 256], U8, name="ws_%d" % c, align_bytes=64)
 
-        live = {}
-
-        def t_bias_cast():
-            nc.vector.tensor_copy(out=bf32[:], in_=brow[:])
-
-        def t_bias_tr():
-            bt = psum.tile([P, 512], F32, tag="bank", bufs=BANKS, name="bt")
-            nc.tensor.transpose(bt[:, 0:P], bf32[:], ident[:])
-            live["bt"] = bt
-
-        def t_bias_out():
-            nc.vector.tensor_copy(out=bias[:], in_=live["bt"][:, 0:16])
-            nc.vector.tensor_scalar(out=bk1[:], in0=bias[:, 0:8], scalar1=1.0, scalar2=None, op0=ALU.add)
-            nc.vector.tensor_scalar(out=nbk[:], in0=bias[:, 0:8], scalar1=-1.0, scalar2=None, op0=ALU.mult)
-
-        def t_xt(tg, a, g):
-            xt = psum.tile([P, 512], F32, tag="bank", bufs=BANKS, name="xt")
+        def x_bank(tg, a, g, idx):
+            xt = psum.tile([P, 512], F32, tag="bank", name="xt")
             for aa in range(2):
                 words = x_sb[tg * 4 + a * 2 + aa][:].bitcast(F32)
                 for u in range(2):
-                    nc.tensor.transpose(xt[:, (aa * 2 + u) * P : (aa * 2 + u + 1) * P],
-                                        words[:, 256 * g + u : 256 * (g + 1) : 2], ident[:])
-            live[("xt", tg, a, g)] = xt
-
-        def t_xc(eng, tg, a, g):
+                    nc.tensor.transpose(
+                        xt[:, (aa * 2 + u) * P : (aa * 2 + u + 1) * P],
+                        words[:, 256 * g + u : 256 * (g + 1) : 2],
+                        ident[:],
+                    )
             dst = xg[(tg, g)][:].bitcast(F32)[:, a * 512 : (a + 1) * 512].rearrange("p (a r u) -> p a r u", a=2, u=2)
-            src = live[("xt", tg, a, g)][:].rearrange("p (a u r) -> p a r u", a=2, u=2)
-            if eng == "V":
+            src = xt[:].rearrange("p (a u r) -> p a r u", a=2, u=2)
+            if idx in XV:
                 nc.vector.tensor_copy(out=dst, in_=src)
             else:
                 nc.scalar.copy(out=dst, in_=src)
 
-        def t_xq(tg, g, a0, na):
+        def x_quant(tg, a, g):
             nc.vector.quantize_mx(
-                out=xc[(tg, g)][:, a0 * 256 : (a0 + na) * 256].bitcast(FP8X4),
-                scales=xs[(tg, g)][:, a0 * 256 : (a0 + na) * 256],
-                in_=xg[(tg, g)][:, a0 * 1024 : (a0 + na) * 1024],
+                out=xc[(tg, g)][:, a * 256 : (a + 1) * 256].bitcast(FP8X4),
+                scales=xs[(tg, g)][:, a * 256 : (a + 1) * 256],
+                in_=xg[(tg, g)][:, a * 1024 : (a + 1) * 1024],
             )
 
-        def t_wd(eng, c, q):
-            src = raw[(c, q)]
-            dst = wg[c][:, q, :].rearrange("p (c j) -> p c j", j=4)
-            if eng == "V":
-                nc.vector.tensor_copy(out=dst, in_=src.rearrange("p j c -> p c j"))
-            elif eng == "S":
-                nc.scalar.copy(out=dst[:, 0:CS, :], in_=src[:, :, 0:CS].rearrange("p j c -> p c j"))
-            else:
-                nc.gpsimd.tensor_scalar(out=dst[:, CS:256, :], in0=src[:, :, CS:256].rearrange("p j c -> p c j"),
-                                        scalar1=1.0, scalar2=0.0, op0=ALU.mult, op1=ALU.add)
-
-        def t_wq(c, q0, nq):
-            nc.vector.quantize_mx(
-                out=wc[c][:, q0 : q0 + nq, :].rearrange("p q c -> p (q c)").bitcast(FP8X4),
-                scales=ws[c][:, q0 : q0 + nq, :].rearrange("p q c -> p (q c)"),
-                in_=wg[c][:, q0 : q0 + nq, :].rearrange("p q c -> p (q c)"),
-            )
-
-        def t_mx(n, m):
-            ht, tg = PAIRS[n]
-            c, hh = divmod(ht, 2)
-            t = psum.tile([P, 512], F32, tag="bank", bufs=BANKS, name="acc")
-            for g in range(2):
-                nc.tensor.matmul_mx(
-                    out=t[:],
-                    lhsT=wc[c][:, m * 2 + g, hh * P : (hh + 1) * P].bitcast(FP8X4),
-                    lhsT_scale=ws[c][:, m * 2 + g, hh * P : (hh + 1) * P],
-                    rhs=xc[(tg, g)][:].bitcast(FP8X4),
-                    rhs_scale=xs[(tg, g)][:],
-                    start=(g == 0), stop=(g == 1),
-                )
-            live[("acc", n, m)] = t
-
-        def t_exp(n):
-            ht = PAIRS[n][0]
-            e = work.tile([P, 512], F32, name="e")
-            nc.scalar.activation(out=e[:], in_=live[("acc", n, 0)][:], func=ACT.Exp, bias=bias[:, ht : ht + 1], scale=1.0)
-            live[("e", n)] = e
-
-        def t_d_scalar(n):
-            ht, tg = PAIRS[n]
-            rn = work.tile([P, 512], F32, name="rn")
-            nc.scalar.activation(out=rn[:], in_=live[("acc", n, 0)][:], func=ACT.Relu, bias=nbk[:, ht : ht + 1], scale=-1.0)
-            ec = work.tile([P, 512], F32, name="ec")
-            r = work.tile([P, 512], F32, name="r")
-            for h in range(2):
-                col = (tg * 2 + h) * 8 + ht
-                cols = slice(h * S, (h + 1) * S)
-                nc.scalar.activation(out=r[:, cols], in_=live[("acc", n, 0)][:, cols], func=ACT.Relu, bias=bias[:, ht : ht + 1],
-                                     scale=1.0, accum_out=s_r[:, col : col + 1])
-            for h in range(2):
-                col = (tg * 2 + h) * 8 + ht
-                cols = slice(h * S, (h + 1) * S)
-                nc.scalar.activation(out=ec[:, cols], in_=rn[:, cols], func=ACT.Exp, scale=-1.0, accum_out=s_e[:, col : col + 1])
-            live[("ec", n)] = ec
-            live[("r", n)] = r
-
-        def t_d_add(n):
-            k = work.tile([P, 512], F32, name="k")
-            nc.gpsimd.tensor_tensor(out=k[:], in0=live[("ec", n)][:], in1=live[("r", n)][:], op=ALU.add)
-            live[("k", n)] = k
-
-        def t_dsum():
-            nc.vector.tensor_tensor(out=s_e[:], in0=s_e[:], in1=s_r[:], op=ALU.add)
-
-        def t_dres():
-            nc.vector.tensor_tensor(out=res[:, 32:64], in0=res[:, 32:64], in1=s_e[:], op=ALU.add)
-
-        def t_clamp(n):
-            ec = work.tile([P, 512], F32, name="ec")
-            nc.gpsimd.tensor_scalar(out=ec[:], in0=live[("e", n)][:], scalar1=1.0, scalar2=0.0, op0=ALU.min, op1=ALU.max)
-            live[("ec", n)] = ec
-
-        def t_vk(n):
-            ht, tg = PAIRS[n]
-            k = work.tile([P, 512], F32, name="k")
-            for h in range(2):
-                col = 32 + (tg * 2 + h) * 8 + ht
-                cols = slice(h * S, (h + 1) * S)
-                nc.vector.scalar_tensor_tensor(out=k[:, cols], in0=live[("acc", n, 0)][:, cols], scalar=bk1[:, ht : ht + 1],
-                                               in1=live[("ec", n)][:, cols], op0=ALU.add, op1=ALU.max,
-                                               accum_out=res[:, col : col + 1])
-            live[("k", n)] = k
-
-        def t_vp(n):
-            ht, tg = PAIRS[n]
-            j = work.tile([P, 512], F32, name="j")
-            for h in range(2):
-                col = (tg * 2 + h) * 8 + ht
-                cols = slice(h * S, (h + 1) * S)
-                nc.vector.scalar_tensor_tensor(out=j[:, cols], in0=live[("acc", n, 1)][:, cols], scalar=bias[:, 8 + ht : 9 + ht],
-                                               in1=live[("k", n)][:, cols], op0=ALU.add, op1=ALU.mult,
-                                               accum_out=res[:, col : col + 1])
-
-        tasks = {}
-        text = []
-
-        def add(key, eng, fn, args, deps):
-            tasks[key] = (eng, fn, args, deps)
-            text.append(key)
-
-        def fe_x(tg, engs, fine):
+        idx = 0
+        for tg in range(2):
             for a in range(2):
                 for g in range(2):
-                    add("xt%d%d%d" % (tg, a, g), "T", t_xt, (tg, a, g), [])
-                    add("xc%d%d%d" % (tg, a, g), engs[a * 2 + g], t_xc, (engs[a * 2 + g], tg, a, g), ["xt%d%d%d" % (tg, a, g)])
-                if fine:
-                    for g in range(2):
-                        add("xq%d%d%d" % (tg, g, a), "V", t_xq, (tg, g, a, 1), ["xc%d%d%d" % (tg, a, g)])
-            if not fine:
+                    x_bank(tg, a, g, idx)
+                    idx += 1
                 for g in range(2):
-                    add("xq%d%d" % (tg, g), "V", t_xq, (tg, g, 0, 2), ["xc%d%d%d" % (tg, a, g) for a in range(2)])
+                    x_quant(tg, a, g)
 
-        def fe_w(c, fine):
-            for q in range(4):
-                if (c, q) in VUNITS:
-                    add("wdS%d%d" % (c, q), "V", t_wd, ("V", c, q), [])
-                    add("wdG%d%d" % (c, q), "V", mark, (None,), [])
-                else:
-                    add("wdS%d%d" % (c, q), "S", t_wd, ("S", c, q), [])
-                    add("wdG%d%d" % (c, q), "G", t_wd, ("G", c, q), [])
-                got = ["wdS%d%d" % (c, q), "wdG%d%d" % (c, q)]
-                if fine:
-                    add("wq%d%d" % (c, q), "V", t_wq, (c, q, 1), got)
-                elif q % 2 == 1:
-                    add("wq%d%d" % (c, q // 2), "V", t_wq, (c, q - 1, 2), got + ["wdS%d%d" % (c, q - 1), "wdG%d%d" % (c, q - 1)])
-
-        FINE_X = (True, False)
-        FINE_W = (True, False, False, False)
-
-        def need(n, m):
-            ht, tg = PAIRS[n]
-            c = ht // 2
-            d = ["xq%d%d%d" % (tg, g, a) for g in range(2) for a in range(2)] if FINE_X[tg] else ["xq%d%d" % (tg, g) for g in range(2)]
-            return d + (["wq%d%d" % (c, m * 2 + g) for g in range(2)] if FINE_W[c] else ["wq%d%d" % (c, m)])
-
-        def pair(n):
+        def pair(ht, tg):
+            cg, c0 = divmod(ht * P, CG)
+            acc = []
             for m in range(2):
-                add("mx%d_%d" % (n, m), "T", t_mx, (n, m), need(n, m))
-            if n in DTYPE:
-                add("ds%d" % n, "S", t_d_scalar, (n,), ["mx%d_0" % n, "bout"])
-                add("vk%d" % n, "G", t_d_add, (n,), ["ds%d" % n])
-            else:
-                add("exp%d" % n, "S", t_exp, (n,), ["mx%d_0" % n, "bout"])
-                add("cl%d" % n, "G", t_clamp, (n,), ["exp%d" % n])
-                add("vk%d" % n, "V", t_vk, (n,), ["cl%d" % n])
-            if n == 15 and len(DTYPE) > 0:
-                add("dsum", "V", t_dsum, (), ["ds%d" % i for i in DTYPE])
-                add("dres", "V", t_dres, (), ["dsum"] + ["vk%d" % i for i in range(16)])
-            add("vp%d" % n, "V", t_vp, (n,), ["vk%d" % n, "mx%d_1" % n])
+                t = psum.tile([P, 512], F32, tag="bank", name="acc")
+                for g in range(2):
+                    nc.tensor.matmul_mx(
+                        out=t[:],
+                        lhsT=wc[(m, g, cg)][:, c0 : c0 + P].bitcast(FP8X4),
+                        lhsT_scale=ws[(m, g, cg)][:, c0 : c0 + P],
+                        rhs=xc[(tg, g)][:].bitcast(FP8X4),
+                        rhs_scale=xs[(tg, g)][:],
+                        start=(g == 0),
+                        stop=(g == 1),
+                    )
+                acc.append(t)
+            e = work.tile([P, 512], F32, name="e")
+            nc.scalar.activation(out=e[:], in_=acc[0][:], func=ACT.Exp, bias=bias[:, ht : ht + 1], scale=1.0)
+            r = work.tile([P, 512], F32, name="r")
+            nc.scalar.activation(out=r[:], in_=acc[0][:], func=ACT.Relu, bias=bias[:, ht : ht + 1], scale=1.0)
+            k = work.tile([P, 512], F32, name="k")
+            j = work.tile([P, 512], F32, name="j")
+            for h in range(2):
+                n = tg * 2 + h
+                cols = slice(h * S, (h + 1) * S)
+                nc.vector.scalar_tensor_tensor(
+                    out=k[:, cols], in0=e[:, cols], scalar=1.0, in1=r[:, cols], op0=ALU.min, op1=ALU.add,
+                    accum_out=res[:, 32 + n * 8 + ht : 32 + n * 8 + ht + 1],
+                )
+            for h in range(2):
+                n = tg * 2 + h
+                cols = slice(h * S, (h + 1) * S)
+                nc.vector.scalar_tensor_tensor(
+                    out=j[:, cols], in0=acc[1][:, cols], scalar=bias[:, 8 + ht : 9 + ht], in1=k[:, cols],
+                    op0=ALU.add, op1=ALU.mult,
+                    accum_out=res[:, n * 8 + ht : n * 8 + ht + 1],
+                )
 
-        add("bcast", "V", t_bias_cast, (), [])
-        add("btr", "T", t_bias_tr, (), ["bcast"])
-        add("bout", "V", t_bias_out, (), ["btr"])
-        fe_x(0, ("S", "S", "S", "S"), FINE_X[0])
-        fe_w(0, FINE_W[0])
-        fe_x(1, ("S", "S", "S", "S"), FINE_X[1])
-        for n in range(16):
-            if n % 4 == 2 and n < 12:
-                fe_w(n // 4 + 1, FINE_W[n // 4 + 1])
-            pair(n)
+        late = 0
+        for ht in range(8):
+            for tg in range(2):
+                pair(ht, tg)
+            if late < 4:
+                interleave_w(units[late][0], units[late][1], 1)
+                quantize_w(units[late][0], units[late][1], 1)
+                late += 1
 
-        for key in text:
-            mark(key)
-            tasks[key][1](*tasks[key][2])
-        mark(None)
-
-        rt = psum.tile([P, 512], F32, tag="bank", bufs=BANKS, name="rt")
+        rt = psum.tile([P, 512], F32, tag="bank", name="rt")
         nc.tensor.transpose(rt[:, 0:P], res[:], ident[:])
         rs = keep.tile([64, P], F32, name="rs")
-        nc.scalar.copy(out=rs[:], in_=rt[0:64, 0:P])
+        nc.vector.tensor_copy(out=rs[:], in_=rt[0:64, 0:P])
         nc.sync.dma_start(out=out_0.rearrange("n (t p) -> (n t) p", p=P), in_=rs[0:32, :])
         nc.scalar.dma_start(out=out_1.rearrange("n (t p) -> (n t) p", p=P), in_=rs[32:64, :])

@@ -17,7 +17,7 @@ TOK = NB * S
 FLOPS = 2 * 2 * TOK * D * H
 
 CG = 512
-CV = (256, 160)
+CV = (256, 320)
 XV = (3, 7)
 
 
@@ -28,7 +28,7 @@ def tile_linearattention_pa_kernel(tc, x, Wk, bk, Wv, bv, out_0, out_1):
 
     with ExitStack() as ctx:
         keep = ctx.enter_context(tc.tile_pool(name="keep", bufs=1))
-        work = ctx.enter_context(tc.tile_pool(name="work", bufs=3))
+        work = ctx.enter_context(tc.tile_pool(name="work", bufs=4))
         psum = ctx.enter_context(tc.psum_pool(name="psum", bufs=8))
 
         warm = keep.tile([P, 1], F32, name="warm")
@@ -104,6 +104,10 @@ def tile_linearattention_pa_kernel(tc, x, Wk, bk, Wv, bv, out_0, out_1):
         nc.tensor.transpose(bt[:, 0:P], bf32[:], ident[:])
         bias = keep.tile([P, 16], F32, name="bias")
         nc.vector.tensor_copy(out=bias[:], in_=bt[:, 0:16])
+        bias1 = keep.tile([P, 8], F32, name="bias1")
+        nc.vector.tensor_scalar_add(out=bias1[:], in0=bias[:, 0:8], scalar1=1.0)
+        nbias = keep.tile([P, 8], F32, name="nbias")
+        nc.vector.tensor_scalar_mul(out=nbias[:], in0=bias[:, 0:8], scalar1=-1.0)
 
         xg = {}
         xc = {}
@@ -164,18 +168,34 @@ def tile_linearattention_pa_kernel(tc, x, Wk, bk, Wv, bv, out_0, out_1):
                     )
                 acc.append(t)
             e = work.tile([P, 512], F32, name="e")
-            nc.scalar.activation(out=e[:], in_=acc[0][:], func=ACT.Exp, bias=bias[:, ht : ht + 1], scale=1.0)
             r = work.tile([P, 512], F32, name="r")
-            nc.scalar.activation(out=r[:], in_=acc[0][:], func=ACT.Relu, bias=bias[:, ht : ht + 1], scale=1.0)
             k = work.tile([P, 512], F32, name="k")
             j = work.tile([P, 512], F32, name="j")
-            for h in range(2):
-                n = tg * 2 + h
-                cols = slice(h * S, (h + 1) * S)
-                nc.vector.scalar_tensor_tensor(
-                    out=k[:, cols], in0=e[:, cols], scalar=1.0, in1=r[:, cols], op0=ALU.min, op1=ALU.add,
-                    accum_out=res[:, 32 + n * 8 + ht : 32 + n * 8 + ht + 1],
-                )
+            if tg == 0:
+                t = work.tile([P, 512], F32, name="t")
+                nc.scalar.activation(out=t[:], in_=acc[0][:], func=ACT.Relu, bias=nbias[:, ht : ht + 1], scale=-1.0)
+                for h in range(2):
+                    n = tg * 2 + h
+                    cols = slice(h * S, (h + 1) * S)
+                    nc.scalar.activation(out=r[:, cols], in_=acc[0][:, cols], func=ACT.Relu, bias=bias[:, ht : ht + 1],
+                                         scale=1.0, accum_out=res[:, 64 + n * 8 + ht : 64 + n * 8 + ht + 1])
+                for h in range(2):
+                    n = tg * 2 + h
+                    cols = slice(h * S, (h + 1) * S)
+                    nc.scalar.activation(out=e[:, cols], in_=t[:, cols], func=ACT.Exp, scale=-1.0,
+                                         accum_out=res[:, 32 + n * 8 + ht : 32 + n * 8 + ht + 1])
+                nc.gpsimd.tensor_tensor(out=k[:], in0=e[:], in1=r[:], op=ALU.add)
+            else:
+                nc.scalar.activation(out=e[:], in_=acc[0][:], func=ACT.Exp, bias=bias[:, ht : ht + 1], scale=1.0)
+                nc.gpsimd.tensor_scalar(out=r[:], in0=e[:], scalar1=1.0, scalar2=0.0, op0=ALU.min, op1=ALU.max)
+                for h in range(2):
+                    n = tg * 2 + h
+                    cols = slice(h * S, (h + 1) * S)
+                    nc.vector.scalar_tensor_tensor(
+                        out=k[:, cols], in0=acc[0][:, cols], scalar=bias1[:, ht : ht + 1], in1=r[:, cols],
+                        op0=ALU.add, op1=ALU.max,
+                        accum_out=res[:, 32 + n * 8 + ht : 32 + n * 8 + ht + 1],
+                    )
             for h in range(2):
                 n = tg * 2 + h
                 cols = slice(h * S, (h + 1) * S)
@@ -194,6 +214,7 @@ def tile_linearattention_pa_kernel(tc, x, Wk, bk, Wv, bv, out_0, out_1):
                 quantize_w(units[late][0], units[late][1], 1)
                 late += 1
 
+        nc.vector.tensor_tensor(out=res[:, 32:48], in0=res[:, 32:48], in1=res[:, 64:80], op=ALU.add)
         rt = psum.tile([P, 512], F32, tag="bank", name="rt")
         nc.tensor.transpose(rt[:, 0:P], res[:], ident[:])
         rs = keep.tile([64, P], F32, name="rs")

@@ -171,7 +171,7 @@ def tile_linearattention_pa_kernel(tc, x, Wk, bk, Wv, bv, out_0, out_1):
             r = work.tile([P, 512], F32, name="r")
             k = work.tile([P, 512], F32, name="k")
             j = work.tile([P, 512], F32, name="j")
-            if tg == 0:
+            if tg == 1:
                 t = work.tile([P, 512], F32, name="t")
                 nc.scalar.activation(out=t[:], in_=acc[0][:], func=ACT.Relu, bias=nbias[:, ht : ht + 1], scale=-1.0)
                 for h in range(2):
@@ -179,12 +179,12 @@ def tile_linearattention_pa_kernel(tc, x, Wk, bk, Wv, bv, out_0, out_1):
                     cols = slice(h * S, (h + 1) * S)
                     nc.scalar.activation(out=r[:, cols], in_=acc[0][:, cols], func=ACT.Relu, bias=bias[:, ht : ht + 1],
                                          scale=1.0, accum_out=res[:, 64 + n * 8 + ht : 64 + n * 8 + ht + 1])
-                for h in range(2):
-                    n = tg * 2 + h
-                    cols = slice(h * S, (h + 1) * S)
                     nc.scalar.activation(out=e[:, cols], in_=t[:, cols], func=ACT.Exp, scale=-1.0,
                                          accum_out=res[:, 32 + n * 8 + ht : 32 + n * 8 + ht + 1])
-                nc.gpsimd.tensor_tensor(out=k[:], in0=e[:], in1=r[:], op=ALU.add)
+                    if ht == 7:
+                        nc.gpsimd.tensor_tensor(out=k[:, cols], in0=e[:, cols], in1=r[:, cols], op=ALU.add)
+                if ht < 7:
+                    nc.gpsimd.tensor_tensor(out=k[:], in0=e[:], in1=r[:], op=ALU.add)
             else:
                 nc.scalar.activation(out=e[:], in_=acc[0][:], func=ACT.Exp, bias=bias[:, ht : ht + 1], scale=1.0)
                 nc.gpsimd.tensor_scalar(out=r[:], in0=e[:], scalar1=1.0, scalar2=0.0, op0=ALU.min, op1=ALU.max)
@@ -196,6 +196,8 @@ def tile_linearattention_pa_kernel(tc, x, Wk, bk, Wv, bv, out_0, out_1):
                         op0=ALU.add, op1=ALU.max,
                         accum_out=res[:, 32 + n * 8 + ht : 32 + n * 8 + ht + 1],
                     )
+            if (ht, tg) == (7, 1):
+                nc.vector.tensor_tensor(out=res[:, 48:64], in0=res[:, 48:64], in1=res[:, 80:96], op=ALU.add)
             for h in range(2):
                 n = tg * 2 + h
                 cols = slice(h * S, (h + 1) * S)
@@ -214,7 +216,6 @@ def tile_linearattention_pa_kernel(tc, x, Wk, bk, Wv, bv, out_0, out_1):
                 quantize_w(units[late][0], units[late][1], 1)
                 late += 1
 
-        nc.vector.tensor_tensor(out=res[:, 32:48], in0=res[:, 32:48], in1=res[:, 64:80], op=ALU.add)
         rt = psum.tile([P, 512], F32, tag="bank", name="rt")
         nc.tensor.transpose(rt[:, 0:P], res[:], ident[:])
         rs = keep.tile([64, P], F32, name="rs")

@@ -17,7 +17,7 @@ TOK = NB * S
 FLOPS = 2 * 2 * TOK * D * H
 
 CG = 512
-CV = (256, 320)
+CV = (256, 272)
 XV = (3, 7)
 
 

@@ -17,8 +17,10 @@ TOK = NB * S
 FLOPS = 2 * 2 * TOK * D * H
 
 CG = 512
-CV = (256, 272)
+CV = 256
 XV = (3, 7)
+W_LATE_AFTER = 2
+X1_AFTER = 3
 
 
 def tile_linearattention_pa_kernel(tc, x, Wk, bk, Wv, bv, out_0, out_1):
@@ -48,35 +50,44 @@ def tile_linearattention_pa_kernel(tc, x, Wk, bk, Wv, bv, out_0, out_1):
         raw = {}
         x_sb = {}
 
-        def load_w(cg):
-            for g in range(2):
-                for m in range(2):
-                    t = keep.tile([P, 4, CG], BF16, name="raw_%d_%d_%d" % (m, g, cg))
-                    nc.sync.dma_start(
-                        out=t[:],
-                        in_=W[m][g * 512 : (g + 1) * 512, cg * CG : (cg + 1) * CG].rearrange("(p j) c -> p j c", j=4),
-                    )
-                    raw[(m, g, cg)] = t
+        def load_w(m, g, pieces):
+            wd = H // pieces
+            for c in range(pieces):
+                t = keep.tile([P, 4, wd], BF16, name="raw_%d_%d_%d" % (m, g, c))
+                nc.sync.dma_start(
+                    out=t[:],
+                    in_=W[m][g * 512 : (g + 1) * 512, c * wd : (c + 1) * wd].rearrange("(p j) c -> p j c", j=4),
+                )
+                for cc in range(wd // CG):
+                    raw[(m, g, c * (wd // CG) + cc)] = t[:, :, cc * CG : (cc + 1) * CG]
 
-        load_w(0)
-        for r in range(8):
-            t = keep.tile([P, D], BF16, name="x_%d" % r)
-            nc.sync.dma_start(out=t[:], in_=xf[r * P : (r + 1) * P, :])
-            x_sb[r] = t
-        load_w(1)
+        def load_x(n):
+            t = keep.tile([P, 2, D], BF16, name="x_%d" % n)
+            nc.sync.dma_start(out=t[:], in_=xf[n * S : (n + 1) * S, :].rearrange("(p a) d -> p a d", a=2))
+            for a in range(2):
+                x_sb[2 * n + a] = t[:, a, :]
+
+        halves = [(m, g) for g in range(2) for m in range(2)]
+        load_w(halves[0][0], halves[0][1], 2)
+        load_w(halves[1][0], halves[1][1], 1)
+        load_x(0)
+        load_x(1)
+        load_w(halves[2][0], halves[2][1], 1)
+        load_w(halves[3][0], halves[3][1], 1)
+        load_x(2)
+        load_x(3)
 
         wg = {}
         wc = {}
         ws = {}
 
         def interleave_w(m, g, cg):
-            cv = CV[cg]
             t = keep.tile([P, CG, 4], BF16, name="wg_%d_%d_%d" % (m, g, cg), align_bytes=64)
             src = raw[(m, g, cg)]
-            nc.vector.tensor_copy(out=t[:, 0:cv, :].rearrange("p (c i) j -> p c j i", i=4),
-                                  in_=src[:, :, 0:cv].rearrange("p j (c i) -> p c j i", i=4))
-            nc.scalar.copy(out=t[:, cv:CG, :].rearrange("p (c i) j -> p c j i", i=4),
-                           in_=src[:, :, cv:CG].rearrange("p j (c i) -> p c j i", i=4))
+            nc.vector.tensor_copy(out=t[:, 0:CV, :].rearrange("p (c i) j -> p c j i", i=4),
+                                  in_=src[:, :, 0:CV].rearrange("p j (c i) -> p c j i", i=4))
+            nc.scalar.copy(out=t[:, CV:CG, :].rearrange("p (c i) j -> p c j i", i=4),
+                           in_=src[:, :, CV:CG].rearrange("p j (c i) -> p c j i", i=4))
             wg[(m, g, cg)] = t
 
         def quantize_w(m, g, cg):
@@ -90,25 +101,6 @@ def tile_linearattention_pa_kernel(tc, x, Wk, bk, Wv, bv, out_0, out_1):
             wc[(m, g, cg)] = codes
             ws[(m, g, cg)] = scales
 
-        units = [(m, g) for g in range(2) for m in range(2)]
-
-        interleave_w(units[0][0], units[0][1], 0)
-        for i in range(1, 4):
-            interleave_w(units[i][0], units[i][1], 0)
-            quantize_w(units[i - 1][0], units[i - 1][1], 0)
-        quantize_w(units[3][0], units[3][1], 0)
-
-        bf32 = keep.tile([P, P], F32, name="bf32")
-        nc.vector.tensor_copy(out=bf32[:], in_=brow[:])
-        bt = psum.tile([P, 512], F32, tag="bank", name="bt")
-        nc.tensor.transpose(bt[:, 0:P], bf32[:], ident[:])
-        bias = keep.tile([P, 16], F32, name="bias")
-        nc.vector.tensor_copy(out=bias[:], in_=bt[:, 0:16])
-        bias1 = keep.tile([P, 8], F32, name="bias1")
-        nc.vector.tensor_scalar_add(out=bias1[:], in0=bias[:, 0:8], scalar1=1.0)
-        nbias = keep.tile([P, 8], F32, name="nbias")
-        nc.vector.tensor_scalar_mul(out=nbias[:], in0=bias[:, 0:8], scalar1=-1.0)
-
         xg = {}
         xc = {}
         xs = {}
@@ -118,10 +110,10 @@ def tile_linearattention_pa_kernel(tc, x, Wk, bk, Wv, bv, out_0, out_1):
                 xc[(tg, g)] = keep.tile([P, 512], U32, name="xc_%d_%d" % (tg, g), align_bytes=64)
                 xs[(tg, g)] = keep.tile([P, 512], U8, name="xs_%d_%d" % (tg, g), align_bytes=64)
 
-        def x_bank(tg, a, g, idx):
+        def x_bank(tg, a, g):
             xt = psum.tile([P, 512], F32, tag="bank", name="xt")
             for aa in range(2):
-                words = x_sb[tg * 4 + a * 2 + aa][:].bitcast(F32)
+                words = x_sb[tg * 4 + a * 2 + aa].bitcast(F32)
                 for u in range(2):
                     nc.tensor.transpose(
                         xt[:, (aa * 2 + u) * P : (aa * 2 + u + 1) * P],
@@ -130,7 +122,7 @@ def tile_linearattention_pa_kernel(tc, x, Wk, bk, Wv, bv, out_0, out_1):
                     )
             dst = xg[(tg, g)][:].bitcast(F32)[:, a * 512 : (a + 1) * 512].rearrange("p (a r u) -> p a r u", a=2, u=2)
             src = xt[:].rearrange("p (a u r) -> p a r u", a=2, u=2)
-            if idx in XV:
+            if tg * 4 + a * 2 + g in XV:
                 nc.vector.tensor_copy(out=dst, in_=src)
             else:
                 nc.scalar.copy(out=dst, in_=src)
@@ -142,16 +134,41 @@ def tile_linearattention_pa_kernel(tc, x, Wk, bk, Wv, bv, out_0, out_1):
                 in_=xg[(tg, g)][:, a * 1024 : (a + 1) * 1024],
             )
 
-        idx = 0
-        for tg in range(2):
+        def x_half(tg):
             for a in range(2):
                 for g in range(2):
-                    x_bank(tg, a, g, idx)
-                    idx += 1
+                    x_bank(tg, a, g)
                 for g in range(2):
                     x_quant(tg, a, g)
 
-        def pair(ht, tg):
+        def biases():
+            bf32 = keep.tile([P, P], F32, name="bf32")
+            nc.vector.tensor_copy(out=bf32[:], in_=brow[:])
+            bt = psum.tile([P, 512], F32, tag="bank", name="bt")
+            nc.tensor.transpose(bt[:, 0:P], bf32[:], ident[:])
+            nc.vector.tensor_copy(out=bias[:], in_=bt[:, 0:16])
+            nc.vector.tensor_scalar_add(out=bias1[:], in0=bias[:, 0:8], scalar1=1.0)
+            nc.vector.tensor_scalar_mul(out=nbias[:], in0=bias[:, 0:8], scalar1=-1.0)
+
+        bias = keep.tile([P, 16], F32, name="bias")
+        bias1 = keep.tile([P, 8], F32, name="bias1")
+        nbias = keep.tile([P, 8], F32, name="nbias")
+
+        units = [(m, g, cg) for (m, g) in halves for cg in range(2)]
+        interleave_w(*units[0])
+        for i in range(1, 4):
+            interleave_w(*units[i])
+            quantize_w(*units[i - 1])
+        quantize_w(*units[3])
+        x_half(0)
+        biases()
+        interleave_w(*units[4])
+        for i in range(5, 7):
+            interleave_w(*units[i])
+            quantize_w(*units[i - 1])
+        quantize_w(*units[6])
+
+        def pair(ht, tg, last):
             cg, c0 = divmod(ht * P, CG)
             acc = []
             for m in range(2):
@@ -171,7 +188,7 @@ def tile_linearattention_pa_kernel(tc, x, Wk, bk, Wv, bv, out_0, out_1):
             r = work.tile([P, 512], F32, name="r")
             k = work.tile([P, 512], F32, name="k")
             j = work.tile([P, 512], F32, name="j")
-            if tg == 1:
+            if ht % 2 == 1:
                 t = work.tile([P, 512], F32, name="t")
                 nc.scalar.activation(out=t[:], in_=acc[0][:], func=ACT.Relu, bias=nbias[:, ht : ht + 1], scale=-1.0)
                 for h in range(2):
@@ -181,9 +198,9 @@ def tile_linearattention_pa_kernel(tc, x, Wk, bk, Wv, bv, out_0, out_1):
                                          scale=1.0, accum_out=res[:, 64 + n * 8 + ht : 64 + n * 8 + ht + 1])
                     nc.scalar.activation(out=e[:, cols], in_=t[:, cols], func=ACT.Exp, scale=-1.0,
                                          accum_out=res[:, 32 + n * 8 + ht : 32 + n * 8 + ht + 1])
-                    if ht == 7:
+                    if last:
                         nc.gpsimd.tensor_tensor(out=k[:, cols], in0=e[:, cols], in1=r[:, cols], op=ALU.add)
-                if ht < 7:
+                if not last:
                     nc.gpsimd.tensor_tensor(out=k[:], in0=e[:], in1=r[:], op=ALU.add)
             else:
                 nc.scalar.activation(out=e[:], in_=acc[0][:], func=ACT.Exp, bias=bias[:, ht : ht + 1], scale=1.0)
@@ -196,8 +213,8 @@ def tile_linearattention_pa_kernel(tc, x, Wk, bk, Wv, bv, out_0, out_1):
                         op0=ALU.add, op1=ALU.max,
                         accum_out=res[:, 32 + n * 8 + ht : 32 + n * 8 + ht + 1],
                     )
-            if (ht, tg) == (7, 1):
-                nc.vector.tensor_tensor(out=res[:, 48:64], in0=res[:, 48:64], in1=res[:, 80:96], op=ALU.add)
+            if last:
+                nc.vector.tensor_tensor(out=res[:, 32:64], in0=res[:, 32:64], in1=res[:, 64:96], op=ALU.add)
             for h in range(2):
                 n = tg * 2 + h
                 cols = slice(h * S, (h + 1) * S)
@@ -207,14 +224,14 @@ def tile_linearattention_pa_kernel(tc, x, Wk, bk, Wv, bv, out_0, out_1):
                     accum_out=res[:, n * 8 + ht : n * 8 + ht + 1],
                 )
 
-        late = 0
-        for ht in range(8):
-            for tg in range(2):
-                pair(ht, tg)
-            if late < 4:
-                interleave_w(units[late][0], units[late][1], 1)
-                quantize_w(units[late][0], units[late][1], 1)
-                late += 1
+        order = [(ht, tg) for tg in range(2) for ht in range(8)]
+        for i in range(16):
+            if i == W_LATE_AFTER:
+                interleave_w(*units[7])
+                quantize_w(*units[7])
+            if i == X1_AFTER:
+                x_half(1)
+            pair(order[i][0], order[i][1], i == 15)
 
         rt = psum.tile([P, 512], F32, tag="bank", name="rt")
         nc.tensor.transpose(rt[:, 0:P], res[:], ident[:])

@@ -18,9 +18,8 @@ FLOPS = 2 * 2 * TOK * D * H
 
 CG = 512
 CV = 256
-XV = (3, 7)
-W_LATE_AFTER = 2
-X1_AFTER = 3
+XV = (1, 3, 7)
+X1_AFTER = 2
 
 
 def tile_linearattention_pa_kernel(tc, x, Wk, bk, Wv, bv, out_0, out_1):
@@ -163,10 +162,10 @@ def tile_linearattention_pa_kernel(tc, x, Wk, bk, Wv, bv, out_0, out_1):
         x_half(0)
         biases()
         interleave_w(*units[4])
-        for i in range(5, 7):
+        for i in range(5, 8):
             interleave_w(*units[i])
             quantize_w(*units[i - 1])
-        quantize_w(*units[6])
+        quantize_w(*units[7])
 
         def pair(ht, tg, last):
             cg, c0 = divmod(ht * P, CG)
@@ -226,9 +225,6 @@ def tile_linearattention_pa_kernel(tc, x, Wk, bk, Wv, bv, out_0, out_1):
 
         order = [(ht, tg) for tg in range(2) for ht in range(8)]
         for i in range(16):
-            if i == W_LATE_AFTER:
-                interleave_w(*units[7])
-                quantize_w(*units[7])
             if i == X1_AFTER:
                 x_half(1)
             pair(order[i][0], order[i][1], i == 15)

@@ -20,6 +20,7 @@ CG = 512
 CV = 256
 XV = (1, 3, 7)
 X1_AFTER = 2
+LAG = 3
 
 
 def tile_linearattention_pa_kernel(tc, x, Wk, bk, Wv, bv, out_0, out_1):
@@ -30,6 +31,7 @@ def tile_linearattention_pa_kernel(tc, x, Wk, bk, Wv, bv, out_0, out_1):
     with ExitStack() as ctx:
         keep = ctx.enter_context(tc.tile_pool(name="keep", bufs=1))
         work = ctx.enter_context(tc.tile_pool(name="work", bufs=4))
+        kpool = ctx.enter_context(tc.tile_pool(name="kpool", bufs=LAG + 3))
         psum = ctx.enter_context(tc.psum_pool(name="psum", bufs=8))
 
         warm = keep.tile([P, 1], F32, name="warm")
@@ -167,33 +169,36 @@ def tile_linearattention_pa_kernel(tc, x, Wk, bk, Wv, bv, out_0, out_1):
             quantize_w(*units[i - 1])
         quantize_w(*units[7])
 
-        def pair(ht, tg, last):
+        def product(m, ht, tg):
             cg, c0 = divmod(ht * P, CG)
-            acc = []
-            for m in range(2):
-                t = psum.tile([P, 512], F32, tag="bank", name="acc")
-                for g in range(2):
-                    nc.tensor.matmul_mx(
-                        out=t[:],
-                        lhsT=wc[(m, g, cg)][:, c0 : c0 + P].bitcast(FP8X4),
-                        lhsT_scale=ws[(m, g, cg)][:, c0 : c0 + P],
-                        rhs=xc[(tg, g)][:].bitcast(FP8X4),
-                        rhs_scale=xs[(tg, g)][:],
-                        start=(g == 0),
-                        stop=(g == 1),
-                    )
-                acc.append(t)
+            t = psum.tile([P, 512], F32, tag="bank", name="acc")
+            for g in range(2):
+                nc.tensor.matmul_mx(
+                    out=t[:],
+                    lhsT=wc[(m, g, cg)][:, c0 : c0 + P].bitcast(FP8X4),
+                    lhsT_scale=ws[(m, g, cg)][:, c0 : c0 + P],
+                    rhs=xc[(tg, g)][:].bitcast(FP8X4),
+                    rhs_scale=xs[(tg, g)][:],
+                    start=(g == 0),
+                    stop=(g == 1),
+                )
+            return t
+
+        kt = {}
+
+        def key_part(ht, tg, last):
+            acc = product(0, ht, tg)
             e = work.tile([P, 512], F32, name="e")
             r = work.tile([P, 512], F32, name="r")
-            k = work.tile([P, 512], F32, name="k")
-            j = work.tile([P, 512], F32, name="j")
+            k = kpool.tile([P, 512], F32, name="k")
+            kt[(ht, tg)] = k
             if ht % 2 == 1:
                 t = work.tile([P, 512], F32, name="t")
-                nc.scalar.activation(out=t[:], in_=acc[0][:], func=ACT.Relu, bias=nbias[:, ht : ht + 1], scale=-1.0)
+                nc.scalar.activation(out=t[:], in_=acc[:], func=ACT.Relu, bias=nbias[:, ht : ht + 1], scale=-1.0)
                 for h in range(2):
                     n = tg * 2 + h
                     cols = slice(h * S, (h + 1) * S)
-                    nc.scalar.activation(out=r[:, cols], in_=acc[0][:, cols], func=ACT.Relu, bias=bias[:, ht : ht + 1],
+                    nc.scalar.activation(out=r[:, cols], in_=acc[:, cols], func=ACT.Relu, bias=bias[:, ht : ht + 1],
                                          scale=1.0, accum_out=res[:, 64 + n * 8 + ht : 64 + n * 8 + ht + 1])
                     nc.scalar.activation(out=e[:, cols], in_=t[:, cols], func=ACT.Exp, scale=-1.0,
                                          accum_out=res[:, 32 + n * 8 + ht : 32 + n * 8 + ht + 1])
@@ -202,32 +207,40 @@ def tile_linearattention_pa_kernel(tc, x, Wk, bk, Wv, bv, out_0, out_1):
                 if not last:
                     nc.gpsimd.tensor_tensor(out=k[:], in0=e[:], in1=r[:], op=ALU.add)
             else:
-                nc.scalar.activation(out=e[:], in_=acc[0][:], func=ACT.Exp, bias=bias[:, ht : ht + 1], scale=1.0)
+                nc.scalar.activation(out=e[:], in_=acc[:], func=ACT.Exp, bias=bias[:, ht : ht + 1], scale=1.0)
                 nc.gpsimd.tensor_scalar(out=r[:], in0=e[:], scalar1=1.0, scalar2=0.0, op0=ALU.min, op1=ALU.max)
                 for h in range(2):
                     n = tg * 2 + h
                     cols = slice(h * S, (h + 1) * S)
                     nc.vector.scalar_tensor_tensor(
-                        out=k[:, cols], in0=acc[0][:, cols], scalar=bias1[:, ht : ht + 1], in1=r[:, cols],
+                        out=k[:, cols], in0=acc[:, cols], scalar=bias1[:, ht : ht + 1], in1=r[:, cols],
                         op0=ALU.add, op1=ALU.max,
                         accum_out=res[:, 32 + n * 8 + ht : 32 + n * 8 + ht + 1],
                     )
+
+        def value_part(ht, tg, last):
+            acc = product(1, ht, tg)
+            k = kt[(ht, tg)]
+            j = work.tile([P, 512], F32, name="j")
             if last:
                 nc.vector.tensor_tensor(out=res[:, 32:64], in0=res[:, 32:64], in1=res[:, 64:96], op=ALU.add)
             for h in range(2):
                 n = tg * 2 + h
                 cols = slice(h * S, (h + 1) * S)
                 nc.vector.scalar_tensor_tensor(
-                    out=j[:, cols], in0=acc[1][:, cols], scalar=bias[:, 8 + ht : 9 + ht], in1=k[:, cols],
+                    out=j[:, cols], in0=acc[:, cols], scalar=bias[:, 8 + ht : 9 + ht], in1=k[:, cols],
                     op0=ALU.add, op1=ALU.mult,
                     accum_out=res[:, n * 8 + ht : n * 8 + ht + 1],
                 )
 
         order = [(ht, tg) for tg in range(2) for ht in range(8)]
-        for i in range(16):
+        for i in range(16 + LAG):
             if i == X1_AFTER:
                 x_half(1)
-            pair(order[i][0], order[i][1], i == 15)
+            if i < 16:
+                key_part(order[i][0], order[i][1], i == 15)
+            if i >= LAG:
+                value_part(order[i - LAG][0], order[i - LAG][1], i - LAG == 15)
 
         rt = psum.tile([P, 512], F32, tag="bank", name="rt")
         nc.tensor.transpose(rt[:, 0:P], res[:], ident[:])

@@ -18,6 +18,7 @@ FLOPS = 2 * 2 * TOK * D * H
 
 CG = 512
 CV = 256
+CV_LAST = 352
 XV = (1, 3, 7)
 X1_AFTER = 2
 LAG = 3
@@ -85,10 +86,11 @@ def tile_linearattention_pa_kernel(tc, x, Wk, bk, Wv, bv, out_0, out_1):
         def interleave_w(m, g, cg):
             t = keep.tile([P, CG, 4], BF16, name="wg_%d_%d_%d" % (m, g, cg), align_bytes=64)
             src = raw[(m, g, cg)]
-            nc.vector.tensor_copy(out=t[:, 0:CV, :].rearrange("p (c i) j -> p c j i", i=4),
-                                  in_=src[:, :, 0:CV].rearrange("p j (c i) -> p c j i", i=4))
-            nc.scalar.copy(out=t[:, CV:CG, :].rearrange("p (c i) j -> p c j i", i=4),
-                           in_=src[:, :, CV:CG].rearrange("p j (c i) -> p c j i", i=4))
+            cv = CV_LAST if (m, g) == halves[3] else CV
+            nc.vector.tensor_copy(out=t[:, 0:cv, :].rearrange("p (c i) j -> p c j i", i=4),
+                                  in_=src[:, :, 0:cv].rearrange("p j (c i) -> p c j i", i=4))
+            nc.scalar.copy(out=t[:, cv:CG, :].rearrange("p (c i) j -> p c j i", i=4),
+                           in_=src[:, :, cv:CG].rearrange("p j (c i) -> p c j i", i=4))
             wg[(m, g, cg)] = t
 
         def quantize_w(m, g, cg):

@@ -18,8 +18,8 @@ FLOPS = 2 * 2 * TOK * D * H
 
 CG = 512
 CV = 256
-CV_LAST = 352
-XV = (1, 3, 7)
+CV_LATE = 352
+XV = (7,)
 X1_AFTER = 2
 LAG = 3
 
@@ -86,7 +86,7 @@ def tile_linearattention_pa_kernel(tc, x, Wk, bk, Wv, bv, out_0, out_1):
         def interleave_w(m, g, cg):
             t = keep.tile([P, CG, 4], BF16, name="wg_%d_%d_%d" % (m, g, cg), align_bytes=64)
             src = raw[(m, g, cg)]
-            cv = CV_LAST if (m, g) == halves[3] else CV
+            cv = CV_LATE if (m, g) in halves[2:4] else CV
             nc.vector.tensor_copy(out=t[:, 0:cv, :].rearrange("p (c i) j -> p c j i", i=4),
                                   in_=src[:, :, 0:cv].rearrange("p j (c i) -> p c j i", i=4))
             nc.scalar.copy(out=t[:, cv:CG, :].rearrange("p (c i) j -> p c j i", i=4),

@@ -21,6 +21,7 @@ CV = 256
 CV_LATE = 352
 XV = (7,)
 X1_AFTER = 2
+NWARM = 3
 LAG = 3
 
 
@@ -170,6 +171,9 @@ def tile_linearattention_pa_kernel(tc, x, Wk, bk, Wv, bv, out_0, out_1):
             interleave_w(*units[i])
             quantize_w(*units[i - 1])
         quantize_w(*units[7])
+        dummy = psum.tile([P, 512], F32, tag="bank", name="dummy")
+        for i in range(NWARM):
+            nc.tensor.matmul(out=dummy[:], lhsT=raw[units[4]][:, 0, 0:P], rhs=raw[units[4]][:, 1, :], start=True, stop=True)
 
         def product(m, ht, tg):
             cg, c0 = divmod(ht * P, CG)

@@ -47,8 +47,9 @@ def tile_linearattention_pa_kernel(tc, x, Wk, bk, Wv, bv, out_0, out_1):
         nc.scalar.dma_start(out=brow[8:16, :], in_=bv.rearrange("(t p) -> t p", p=P))
         ident = keep.tile([P, P], F32, name="ident")
         make_identity(nc, ident[:])
-        res = keep.tile([P, P], F32, name="res")
+        res = keep.tile([P, P], F32, name="res", align_bytes=64)
         nc.vector.memset(res[:], 0.0)
+        resT = keep.tile([P, 64], F32, name="resT", align_bytes=64)
 
         raw = {}
         x_sb = {}
@@ -230,6 +231,7 @@ def tile_linearattention_pa_kernel(tc, x, Wk, bk, Wv, bv, out_0, out_1):
             j = work.tile([P, 512], F32, name="j")
             if last:
                 nc.vector.tensor_tensor(out=res[:, 32:64], in0=res[:, 32:64], in1=res[:, 64:96], op=ALU.add)
+                store(out_1, 1, (nc.sync, nc.sync, nc.sync, nc.sync))
             for h in range(2):
                 n = tg * 2 + h
                 cols = slice(h * S, (h + 1) * S)
@@ -238,6 +240,12 @@ def tile_linearattention_pa_kernel(tc, x, Wk, bk, Wv, bv, out_0, out_1):
                     op0=ALU.add, op1=ALU.mult,
                     accum_out=res[:, n * 8 + ht : n * 8 + ht + 1],
                 )
+
+        def store(dst, b, queues):
+            nc.vector.transpose(out=resT[:, 32 * b : 32 * b + 32], in_=res[:, 32 * b : 32 * b + 32])
+            view = dst.rearrange("n (t a j) -> a (n t) j", a=4, j=32)
+            for a in range(4):
+                queues[a].dma_start(out=view[a], in_=resT[32 * a : 32 * a + 32, 32 * b : 32 * b + 32])
 
         order = [(ht, tg) for tg in range(2) for ht in range(8)]
         for i in range(16 + LAG):
@@ -248,9 +256,4 @@ def tile_linearattention_pa_kernel(tc, x, Wk, bk, Wv, bv, out_0, out_1):
             if i >= LAG:
                 value_part(order[i - LAG][0], order[i - LAG][1], i - LAG == 15)
 
-        rt = psum.tile([P, 512], F32, tag="bank", name="rt")
-        nc.tensor.transpose(rt[:, 0:P], res[:], ident[:])
-        rs = keep.tile([64, P], F32, name="rs")
-        nc.vector.tensor_copy(out=rs[:], in_=rt[0:64, 0:P])
-        nc.sync.dma_start(out=out_0.rearrange("n (t p) -> (n t) p", p=P), in_=rs[0:32, :])
-        nc.scalar.dma_start(out=out_1.rearrange("n (t p) -> (n t) p", p=P), in_=rs[32:64, :])
+        store(out_0, 0, (nc.sync, nc.scalar, nc.sync, nc.scalar))

@@ -17,7 +17,7 @@ TOK = NB * S
 FLOPS = 2 * 2 * TOK * D * H
 
 CG = 512
-CV = 256
+CV = 320
 CV_LATE = 352
 XV = (7,)
 X1_AFTER = 2
@@ -72,7 +72,7 @@ def tile_linearattention_pa_kernel(tc, x, Wk, bk, Wv, bv, out_0, out_1):
                 x_sb[2 * n + a] = t[:, a, :]
 
         halves = [(m, g) for g in range(2) for m in range(2)]
-        load_w(halves[0][0], halves[0][1], 2)
+        load_w(halves[0][0], halves[0][1], 1)
         load_w(halves[1][0], halves[1][1], 1)
         load_x(0)
         load_x(1)

@@ -243,9 +243,7 @@ def tile_linearattention_pa_kernel(tc, x, Wk, bk, Wv, bv, out_0, out_1):
 
         def store(dst, b, queues):
             nc.vector.transpose(out=resT[:, 32 * b : 32 * b + 32], in_=res[:, 32 * b : 32 * b + 32])
-            view = dst.rearrange("n (t a j) -> a (n t) j", a=4, j=32)
-            for a in range(4):
-                queues[a].dma_start(out=view[a], in_=resT[32 * a : 32 * a + 32, 32 * b : 32 * b + 32])
+            queues[0].dma_start(out=dst.rearrange("n (t a j) -> a (n t) j", a=4, j=32), in_=resT[:, 32 * b : 32 * b + 32])
 
         order = [(ht, tg) for tg in range(2) for ht in range(8)]
         for i in range(16 + LAG):

@@ -19,6 +19,7 @@ FLOPS = 2 * 2 * TOK * D * H
 CG = 512
 CV = 320
 CV_LATE = 352
+CV_THIRD = 288
 XV = (7,)
 X1_AFTER = 2
 NWARM = 3
@@ -88,7 +89,7 @@ def tile_linearattention_pa_kernel(tc, x, Wk, bk, Wv, bv, out_0, out_1):
         def interleave_w(m, g, cg):
             t = keep.tile([P, CG, 4], BF16, name="wg_%d_%d_%d" % (m, g, cg), align_bytes=64)
             src = raw[(m, g, cg)]
-            cv = CV_LATE if (m, g) in halves[2:4] else CV
+            cv = CV_THIRD if (m, g) == halves[2] else CV_LATE if (m, g) == halves[3] else CV
             nc.vector.tensor_copy(out=t[:, 0:cv, :].rearrange("p (c i) j -> p c j i", i=4),
                                   in_=src[:, :, 0:cv].rearrange("p j (c i) -> p c j i", i=4))
             nc.scalar.copy(out=t[:, cv:CG, :].rearrange("p (c i) j -> p c j i", i=4),

from contextlib import ExitStack

import concourse.mybir as mybir
from concourse.masks import make_identity

F32 = mybir.dt.float32
BF16 = mybir.dt.bfloat16
U32 = mybir.dt.uint32
U8 = mybir.dt.uint8
FP8X4 = mybir.dt.float8_e5m2_x4
ACT = mybir.ActivationFunctionType
ALU = mybir.AluOpType

NB, S, D, H = 4, 256, 1024, 1024
P = 128
TOK = NB * S
FLOPS = 2 * 2 * TOK * D * H

CG = 512
CV = 320
CV_LATE = 352
CV_THIRD = 288
XV = (7,)
X1_AFTER = 2
NWARM = 3
LAG = 3


def tile_linearattention_pa_kernel(tc, x, Wk, bk, Wv, bv, out_0, out_1):
    nc = tc.nc
    W = (Wk, Wv)
    xf = x.flatten_outer_dims()

    with ExitStack() as ctx:
        keep = ctx.enter_context(tc.tile_pool(name="keep", bufs=1))
        work = ctx.enter_context(tc.tile_pool(name="work", bufs=4))
        kpool = ctx.enter_context(tc.tile_pool(name="kpool", bufs=LAG + 3))
        psum = ctx.enter_context(tc.psum_pool(name="psum", bufs=8))

        warm = keep.tile([P, 1], F32, name="warm")
        nc.vector.memset(warm[:], 0.0)
        warm2 = keep.tile([P, 1], F32, name="warm2")
        nc.scalar.activation(out=warm2[:], in_=warm[:], func=ACT.Exp)

        brow = keep.tile([P, P], BF16, name="brow")
        nc.gpsimd.memset(brow[:], 0.0)
        nc.scalar.dma_start(out=brow[0:8, :], in_=bk.rearrange("(t p) -> t p", p=P))
        nc.scalar.dma_start(out=brow[8:16, :], in_=bv.rearrange("(t p) -> t p", p=P))
        ident = keep.tile([P, P], F32, name="ident")
        make_identity(nc, ident[:])
        res = keep.tile([P, P], F32, name="res", align_bytes=64)
        nc.vector.memset(res[:], 0.0)
        resT = keep.tile([P, 64], F32, name="resT", align_bytes=64)

        raw = {}
        x_sb = {}

        def load_w(m, g, pieces):
            wd = H // pieces
            for c in range(pieces):
                t = keep.tile([P, 4, wd], BF16, name="raw_%d_%d_%d" % (m, g, c))
                nc.sync.dma_start(
                    out=t[:],
                    in_=W[m][g * 512 : (g + 1) * 512, c * wd : (c + 1) * wd].rearrange("(p j) c -> p j c", j=4),
                )
                for cc in range(wd // CG):
                    raw[(m, g, c * (wd // CG) + cc)] = t[:, :, cc * CG : (cc + 1) * CG]

        def load_x(n):
            t = keep.tile([P, 2, D], BF16, name="x_%d" % n)
            nc.sync.dma_start(out=t[:], in_=xf[n * S : (n + 1) * S, :].rearrange("(p a) d -> p a d", a=2))
            for a in range(2):
                x_sb[2 * n + a] = t[:, a, :]

        halves = [(m, g) for g in range(2) for m in range(2)]
        load_w(halves[0][0], halves[0][1], 1)
        load_w(halves[1][0], halves[1][1], 1)
        load_x(0)
        load_x(1)
        load_w(halves[2][0], halves[2][1], 1)
        load_w(halves[3][0], halves[3][1], 1)
        load_x(2)
        load_x(3)

        wg = {}
        wc = {}
        ws = {}

        def interleave_w(m, g, cg):
            t = keep.tile([P, CG, 4], BF16, name="wg_%d_%d_%d" % (m, g, cg), align_bytes=64)
            src = raw[(m, g, cg)]
            cv = CV_THIRD if (m, g) == halves[2] else CV_LATE if (m, g) == halves[3] else CV
            nc.vector.tensor_copy(out=t[:, 0:cv, :].rearrange("p (c i) j -> p c j i", i=4),
                                  in_=src[:, :, 0:cv].rearrange("p j (c i) -> p c j i", i=4))
            nc.scalar.copy(out=t[:, cv:CG, :].rearrange("p (c i) j -> p c j i", i=4),
                           in_=src[:, :, cv:CG].rearrange("p j (c i) -> p c j i", i=4))
            wg[(m, g, cg)] = t

        def quantize_w(m, g, cg):
            codes = keep.tile([P, CG], U32, name="wc_%d_%d_%d" % (m, g, cg), align_bytes=64)
            scales = keep.tile([P, CG], U8, name="ws_%d_%d_%d" % (m, g, cg), align_bytes=64)
            nc.vector.quantize_mx(
                out=codes[:].bitcast(FP8X4),
                scales=scales[:],
                in_=wg[(m, g, cg)][:].rearrange("p c j -> p (c j)"),
            )
            wc[(m, g, cg)] = codes
            ws[(m, g, cg)] = scales

        xg = {}
        xc = {}
        xs = {}
        for tg in range(2):
            for g in range(2):
                xg[(tg, g)] = keep.tile([P, 2048], BF16, name="xg_%d_%d" % (tg, g), align_bytes=64)
                xc[(tg, g)] = keep.tile([P, 512], U32, name="xc_%d_%d" % (tg, g), align_bytes=64)
                xs[(tg, g)] = keep.tile([P, 512], U8, name="xs_%d_%d" % (tg, g), align_bytes=64)

        def x_bank(tg, a, g):
            xt = psum.tile([P, 512], F32, tag="bank", name="xt")
            for aa in range(2):
                words = x_sb[tg * 4 + a * 2 + aa].bitcast(F32)
                for u in range(2):
                    nc.tensor.transpose(
                        xt[:, (aa * 2 + u) * P : (aa * 2 + u + 1) * P],
                        words[:, 256 * g + u : 256 * (g + 1) : 2],
                        ident[:],
                    )
            dst = xg[(tg, g)][:].bitcast(F32)[:, a * 512 : (a + 1) * 512].rearrange("p (a r u) -> p a r u", a=2, u=2)
            src = xt[:].rearrange("p (a u r) -> p a r u", a=2, u=2)
            if tg * 4 + a * 2 + g in XV:
                nc.vector.tensor_copy(out=dst, in_=src)
            else:
                nc.scalar.copy(out=dst, in_=src)

        def x_quant(tg, a, g):
            nc.vector.quantize_mx(
                out=xc[(tg, g)][:, a * 256 : (a + 1) * 256].bitcast(FP8X4),
                scales=xs[(tg, g)][:, a * 256 : (a + 1) * 256],
                in_=xg[(tg, g)][:, a * 1024 : (a + 1) * 1024],
            )

        def x_half(tg):
            for a in range(2):
                for g in range(2):
                    x_bank(tg, a, g)
                for g in range(2):
                    x_quant(tg, a, g)

        def biases():
            bf32 = keep.tile([P, P], F32, name="bf32")
            nc.vector.tensor_copy(out=bf32[:], in_=brow[:])
            bt = psum.tile([P, 512], F32, tag="bank", name="bt")
            nc.tensor.transpose(bt[:, 0:P], bf32[:], ident[:])
            nc.vector.tensor_copy(out=bias[:], in_=bt[:, 0:16])
            nc.vector.tensor_scalar_add(out=bias1[:], in0=bias[:, 0:8], scalar1=1.0)
            nc.vector.tensor_scalar_mul(out=nbias[:], in0=bias[:, 0:8], scalar1=-1.0)

        bias = keep.tile([P, 16], F32, name="bias")
        bias1 = keep.tile([P, 8], F32, name="bias1")
        nbias = keep.tile([P, 8], F32, name="nbias")

        units = [(m, g, cg) for (m, g) in halves for cg in range(2)]
        interleave_w(*units[0])
        for i in range(1, 4):
            interleave_w(*units[i])
            quantize_w(*units[i - 1])
        quantize_w(*units[3])
        x_half(0)
        biases()
        interleave_w(*units[4])
        for i in range(5, 8):
            interleave_w(*units[i])
            quantize_w(*units[i - 1])
        quantize_w(*units[7])
        dummy = psum.tile([P, 512], F32, tag="bank", name="dummy")
        for i in range(NWARM):
            nc.tensor.matmul(out=dummy[:], lhsT=raw[units[4]][:, 0, 0:P], rhs=raw[units[4]][:, 1, :], start=True, stop=True)

        def product(m, ht, tg):
            cg, c0 = divmod(ht * P, CG)
            t = psum.tile([P, 512], F32, tag="bank", name="acc")
            for g in range(2):
                nc.tensor.matmul_mx(
                    out=t[:],
                    lhsT=wc[(m, g, cg)][:, c0 : c0 + P].bitcast(FP8X4),
                    lhsT_scale=ws[(m, g, cg)][:, c0 : c0 + P],
                    rhs=xc[(tg, g)][:].bitcast(FP8X4),
                    rhs_scale=xs[(tg, g)][:],
                    start=(g == 0),
                    stop=(g == 1),
                )
            return t

        kt = {}

        def key_part(ht, tg, last):
            acc = product(0, ht, tg)
            e = work.tile([P, 512], F32, name="e")
            r = work.tile([P, 512], F32, name="r")
            k = kpool.tile([P, 512], F32, name="k")
            kt[(ht, tg)] = k
            if ht % 2 == 1:
                t = work.tile([P, 512], F32, name="t")
                nc.scalar.activation(out=t[:], in_=acc[:], func=ACT.Relu, bias=nbias[:, ht : ht + 1], scale=-1.0)
                for h in range(2):
                    n = tg * 2 + h
                    cols = slice(h * S, (h + 1) * S)
                    nc.scalar.activation(out=r[:, cols], in_=acc[:, cols], func=ACT.Relu, bias=bias[:, ht : ht + 1],
                                         scale=1.0, accum_out=res[:, 64 + n * 8 + ht : 64 + n * 8 + ht + 1])
                    nc.scalar.activation(out=e[:, cols], in_=t[:, cols], func=ACT.Exp, scale=-1.0,
                                         accum_out=res[:, 32 + n * 8 + ht : 32 + n * 8 + ht + 1])
                    if last:
                        nc.gpsimd.tensor_tensor(out=k[:, cols], in0=e[:, cols], in1=r[:, cols], op=ALU.add)
                if not last:
                    nc.gpsimd.tensor_tensor(out=k[:], in0=e[:], in1=r[:], op=ALU.add)
            else:
                nc.scalar.activation(out=e[:], in_=acc[:], func=ACT.Exp, bias=bias[:, ht : ht + 1], scale=1.0)
                nc.gpsimd.tensor_scalar(out=r[:], in0=e[:], scalar1=1.0, scalar2=0.0, op0=ALU.min, op1=ALU.max)
                for h in range(2):
                    n = tg * 2 + h
                    cols = slice(h * S, (h + 1) * S)
                    nc.vector.scalar_tensor_tensor(
                        out=k[:, cols], in0=acc[:, cols], scalar=bias1[:, ht : ht + 1], in1=r[:, cols],
                        op0=ALU.add, op1=ALU.max,
                        accum_out=res[:, 32 + n * 8 + ht : 32 + n * 8 + ht + 1],
                    )

        def value_part(ht, tg, last):
            acc = product(1, ht, tg)
            k = kt[(ht, tg)]
            j = work.tile([P, 512], F32, name="j")
            if last:
                nc.vector.tensor_tensor(out=res[:, 32:64], in0=res[:, 32:64], in1=res[:, 64:96], op=ALU.add)
                store(out_1, 1, (nc.sync, nc.sync, nc.sync, nc.sync))
            for h in range(2):
                n = tg * 2 + h
                cols = slice(h * S, (h + 1) * S)
                nc.vector.scalar_tensor_tensor(
                    out=j[:, cols], in0=acc[:, cols], scalar=bias[:, 8 + ht : 9 + ht], in1=k[:, cols],
                    op0=ALU.add, op1=ALU.mult,
                    accum_out=res[:, n * 8 + ht : n * 8 + ht + 1],
                )

        def store(dst, b, queues):
            nc.vector.transpose(out=resT[:, 32 * b : 32 * b + 32], in_=res[:, 32 * b : 32 * b + 32])
            queues[0].dma_start(out=dst.rearrange("n (t a j) -> a (n t) j", a=4, j=32), in_=resT[:, 32 * b : 32 * b + 32])

        order = [(ht, tg) for tg in range(2) for ht in range(8)]
        for i in range(16 + LAG):
            if i == X1_AFTER:
                x_half(1)
            if i < 16:
                key_part(order[i][0], order[i][1], i == 15)
            if i >= LAG:
                value_part(order[i - LAG][0], order[i - LAG][1], i - LAG == 15)

        store(out_0, 0, (nc.sync, nc.scalar, nc.sync, nc.scalar))
